import numpy as np
import ml_dtypes


def mxq(x, axis, fmt="e4m3"):
    dtype, down = {"e4m3": (ml_dtypes.float8_e4m3fn, 7), "e5m2": (ml_dtypes.float8_e5m2, 14)}[fmt]
    v = np.moveaxis(np.asarray(x, np.float32).astype(ml_dtypes.bfloat16).astype(np.float64), axis, -1)
    blocks = v.reshape(v.shape[:-1] + (-1, 32))
    amax = np.abs(blocks).max(-1, keepdims=True)
    byte = np.maximum(np.where(amax > 0, np.frexp(amax)[1] - 1 + 127, 0) - down, 1)
    scale = np.exp2(byte - 127.0)
    codes = (blocks / scale).astype(np.float32).astype(dtype).astype(np.float64)
    return np.moveaxis((codes * scale).reshape(v.shape), -1, axis)


WIDE = False


def mx_kscale(k):
    if not WIDE:
        return np.ones(k)
    levels = np.array([10, -10, 5, -5, 0])
    if k % 512:
        return np.exp2(np.random.permutation(np.resize(levels, k // 32))).repeat(32)
    a = np.empty((k // 512, 16))
    for p in range(k // 512):
        a[p, :8] = np.random.permutation(np.resize(levels, 8))
        for g in range(8):
            far = levels[np.abs(levels - a[p, g]) >= 10]
            a[p, g + 8] = far[np.random.randint(len(far))]
    return np.exp2(a.ravel()).repeat(32)


BF16 = ml_dtypes.bfloat16


def bf(x):
    return np.asarray(x, np.float32).astype(BF16)


def f64(x):
    return np.asarray(x).astype(np.float64)


B, S, H, NH, HD, ROT = 2, 512, 1024, 8, 128, 32
BASE = 10000.0


def rotate_half(x):
    half = x.shape[-1] // 2
    return np.concatenate((-x[..., half:], x[..., :half]), axis=-1)


def rope_tables(seq_len):
    inv_freq = 1.0 / (BASE ** (np.arange(0, ROT, 2) / ROT))
    freqs = np.arange(seq_len)[:, None] * inv_freq[None, :]
    emb = np.concatenate((freqs, freqs), axis=-1)
    return np.cos(emb), np.sin(emb)


def draw0():
    s = mx_kscale(H)
    return {"hidden_states": bf(np.random.standard_normal((B, S, H)) * s),
            "W_qkv": bf(np.random.standard_normal((H, 3 * H)) / np.sqrt(H) / s[:, None]),
            "b_qkv": bf(np.random.standard_normal(3 * H) * 0.3)}


def core(hidden_states, W_qkv, b_qkv):
    qkv = (mxq(f64(hidden_states), 2, "e4m3") @ mxq(f64(W_qkv), 0, "e4m3")) + f64(b_qkv)
    qkv = qkv.reshape(B, S, NH, 3 * HD)
    q = qkv[..., :HD].transpose(0, 2, 1, 3)
    k = qkv[..., HD:2 * HD].transpose(0, 2, 1, 3)
    v = qkv[..., 2 * HD:].transpose(0, 2, 1, 3)
    cos, sin = rope_tables(S)
    q_rot, q_pass = q[..., :ROT], q[..., ROT:]
    k_rot, k_pass = k[..., :ROT], k[..., ROT:]
    q_rot = q_rot * cos + rotate_half(q_rot) * sin
    k_rot = k_rot * cos + rotate_half(k_rot) * sin
    q = np.concatenate((q_rot, q_pass), axis=-1)
    k = np.concatenate((k_rot, k_pass), axis=-1)
    return q, k, np.ascontiguousarray(v)


def e4m3fn_bytes(y):
    return np.clip(np.asarray(y, np.float64), -448.0, 448.0).astype(np.float32).astype(ml_dtypes.float8_e4m3fn).view(np.uint8)


def e4m3fn_values(b):
    return np.asarray(b, np.uint8).view(ml_dtypes.float8_e4m3fn).astype(np.float64)


def setup_inputs():
    d = draw0()
    x0 = np.asarray(d['W_qkv']).astype(np.float64)
    s = (np.max(np.abs(x0), axis=(1,), keepdims=True) / 448.0).astype(np.float32)
    out = {}
    for k, v in d.items():
        if k == 'W_qkv':
            out['W_qkv_bytes'] = e4m3fn_bytes(x0 / s.astype(np.float64))
            out['W_qkv_scale'] = s
        else:
            out[k] = v
    return out


def reference(hidden_states, W_qkv_bytes, W_qkv_scale, b_qkv):
    return core(hidden_states, e4m3fn_values(W_qkv_bytes) * W_qkv_scale.astype(np.float64), b_qkv)

@@ -1,0 +1,332 @@
+from contextlib import ExitStack
+import math
+
+import concourse.mybir as mybir
+from concourse.masks import make_identity
+
+FLOPS = 2 * 1024 * 1024 * 3072
+
+F32 = mybir.dt.float32
+BF16 = mybir.dt.bfloat16
+U32 = mybir.dt.uint32
+U8 = mybir.dt.uint8
+I32 = mybir.dt.int32
+FP8 = mybir.dt.float8_e4m3fn
+FP8X4 = mybir.dt.float8_e4m3fn_x4
+ALU = mybir.AluOpType
+ACT = mybir.ActivationFunctionType
+
+P = 128
+NB = 2
+NJ = 4
+NG = 2
+NC = 6
+CW = 512
+HD = 128
+BASE = 10000.0
+
+PIECES = ((0, 512), (512, 512), (1024, 512), (1536, 512), (2048, 512), (2560, 256), (2816, 256))
+NP = len(PIECES)
+V_COLS = (512, 256, 160, 96, 64, 0, 0)
+ROPE_ON_VECTOR = (4, 5, 6)
+SMALL_ON_VECTOR = (0, 1, 2, 3, 4, 5, 6)
+BYTE_RANGES = ((0, 512), (512, 1024), (1024, 2048), (2048, 3072))
+
+
+def tile_pgtattention_pa_kernel(tc, hidden_states, W_qkv_bytes, W_qkv_scale, b_qkv, out_0, out_1, out_2):
+    nc = tc.nc
+    outs = (out_0, out_1, out_2)
+
+    with ExitStack() as ctx:
+        const = ctx.enter_context(tc.tile_pool(name="const", bufs=1))
+        stage = ctx.enter_context(tc.tile_pool(name="stage", bufs=2))
+        codes = ctx.enter_context(tc.tile_pool(name="codes", bufs=3))
+        scr = ctx.enter_context(tc.tile_pool(name="scr", bufs=2))
+        psum = ctx.enter_context(tc.psum_pool(name="psum", bufs=8))
+
+        wsc = const.tile([P, NG, 4], F32, name="wsc")
+        nc.sync.dma_start(out=wsc[:], in_=W_qkv_scale.rearrange("(g p t) o -> p g (t o)", g=NG, p=P, t=4))
+        wview = W_qkv_bytes.rearrange("(g p t) n -> g p t n", g=NG, p=P, t=4)
+        wbytes = {}
+
+        def load_bytes(r):
+            lo, hi = BYTE_RANGES[r]
+            for g in range(NG):
+                wb = const.tile([P, 4, hi - lo], U8, name="wbytes_%d_%d" % (r, g))
+                nc.sync.dma_start(out=wb[:], in_=wview[g][:, :, lo:hi])
+                wbytes[(r, g)] = wb
+
+        xsb = {}
+
+        def load_x(b):
+            xv = hidden_states[b].rearrange("(p j) k -> p j k", j=NJ)
+            for j in range(NJ):
+                xt = const.tile([P, 1024], BF16, name="xsb_%d_%d" % (b, j))
+                nc.sync.dma_start(out=xt[:], in_=xv[:, j, :])
+                xsb[(b, j)] = xt
+
+        bias_bf = const.tile([P, NC * CW], BF16, name="bias_bf")
+
+        def load_bias(lo, hi):
+            nc.sync.dma_start(out=bias_bf[:, lo:hi], in_=b_qkv[lo:hi].partition_broadcast(P))
+
+        load_bytes(0)
+        load_x(0)
+        load_bias(0, CW)
+        load_bytes(1)
+        load_x(1)
+        load_bias(CW, 2 * CW)
+        load_bytes(2)
+        load_bias(2 * CW, NC * CW)
+        load_bytes(3)
+
+        warm = const.tile([P, 1], F32, name="warm")
+        nc.vector.memset(warm[:], 0.0)
+        warm2 = const.tile([P, 1], F32, name="warm2")
+        nc.scalar.activation(out=warm2[:], in_=warm[:], func=ACT.Sin)
+        ident = const.tile([P, P], F32, name="ident")
+        make_identity(nc, ident[:])
+
+        wide = {}
+        grp = {}
+        wcodes = {}
+
+        def byte_plane(c, g, t):
+            col, width = PIECES[c]
+            for r in range(len(BYTE_RANGES)):
+                lo, hi = BYTE_RANGES[r]
+                if lo <= col < hi:
+                    return wbytes[(r, g)][:, t, col - lo:col + width - lo].bitcast(FP8)
+            return None
+
+        def widen(c, on_vector):
+            width = PIECES[c][1]
+            wd = stage.tile([P, NG, 4, CW], BF16, name="wide_%d" % c, tag="wide")
+            wide[c] = wd
+            for g in range(NG):
+                for t in range(4):
+                    if g in on_vector:
+                        nc.vector.tensor_scalar(out=wd[:, g, t, 0:width], in0=byte_plane(c, g, t),
+                                                scalar1=wsc[:, g, t:t + 1], scalar2=None, op0=ALU.mult)
+                    else:
+                        nc.scalar.activation(out=wd[:, g, t, 0:width], in_=byte_plane(c, g, t), func=ACT.Copy,
+                                             scale=wsc[:, g, t:t + 1])
+
+        def interleave(c, gs):
+            width = PIECES[c][1]
+            wd = wide[c]
+            if c not in grp:
+                grp[c] = stage.tile([P, NG, width, 4], BF16, name="grp_%d" % c, tag="grp", align_bytes=64)
+            gr = grp[c]
+            g0, g1 = gs
+            a = V_COLS[c]
+            if a < width:
+                nc.scalar.copy(out=gr[:, g0:g1, a:width, :],
+                               in_=wd[:, g0:g1, :, a:width].rearrange("p g t n -> p g n t"))
+            if a > 0:
+                nc.vector.tensor_copy(out=gr[:, g0:g1, 0:a, :], in_=wd[:, g0:g1, :, 0:a].rearrange("p g t n -> p g n t"))
+
+        def quant(c, gs):
+            width = PIECES[c][1]
+            if c not in wcodes:
+                wc = codes.tile([P, NG, width], U32, name="wc_%d" % c, tag="wc", align_bytes=64)
+                ws = codes.tile([P, NG, width], U8, name="ws_%d" % c, tag="ws", align_bytes=64)
+                wcodes[c] = (wc, ws)
+            wc, ws = wcodes[c]
+            g0, g1 = gs
+            nc.vector.quantize_mx(out=wc[:, g0:g1, :].rearrange("p g n -> p (g n)").bitcast(FP8X4),
+                                  scales=ws[:, g0:g1, :].rearrange("p g n -> p (g n)"),
+                                  in_=grp[c][:, g0:g1, :, :].rearrange("p g n t -> p (g n t)"))
+
+        xbank = {}
+        xgrp = {}
+        xcodes = {}
+
+        def x_transpose(b, j):
+            bank = psum.tile([P, CW], F32, name="xbank_%d_%d" % (b, j), tag="bank")
+            xbank[(b, j)] = bank
+            words = xsb[(b, j)][:].bitcast(F32)
+            for g in range(NG):
+                for u in range(2):
+                    nc.tensor.transpose(bank[:, (2 * g + u) * P:(2 * g + u + 1) * P],
+                                        words[:, 256 * g + u:256 * (g + 1):2], ident[:])
+
+        def x_evac(b, j):
+            if b not in xgrp:
+                xgrp[b] = const.tile([P, NJ, 1024], BF16, name="xg_%d" % b, align_bytes=64)
+            nc.scalar.copy(out=xgrp[b][:, j, :].bitcast(F32).rearrange("p (g r u) -> p g r u", g=NG, u=2),
+                           in_=xbank[(b, j)][:].rearrange("p (g u r) -> p g r u", g=NG, u=2))
+
+        def x_quant(b, j0):
+            if b not in xcodes:
+                xc = const.tile([P, NJ, 256], U32, name="xc_%d" % b, align_bytes=64)
+                xs = const.tile([P, NJ, 256], U8, name="xs_%d" % b, align_bytes=64)
+                xcodes[b] = (xc, xs)
+            xc, xs = xcodes[b]
+            nc.vector.quantize_mx(out=xc[:, j0:j0 + 2, :].rearrange("p j n -> p (j n)").bitcast(FP8X4),
+                                  scales=xs[:, j0:j0 + 2, :].rearrange("p j n -> p (j n)"),
+                                  in_=xgrp[b][:, j0:j0 + 2, :].rearrange("p j n -> p (j n)"))
+
+        cosf = const.tile([P, NB, 2 * NJ, 32], F32, name="cosf")
+        sinf = const.tile([P, NB, 2 * NJ, 32], F32, name="sinf")
+        two_pi = 2.0 * math.pi
+
+        def small(name):
+            return const.tile([P, NJ, 16], F32, name=name)
+
+        def scaled(dst, src, mul, add):
+            nc.vector.tensor_scalar(out=dst, in0=src, scalar1=mul, scalar2=add, op0=ALU.mult, op1=ALU.add)
+
+        red2 = small("red2")
+        ang = small("ang")
+        turn = small("turn")
+
+        def rope_angles():
+            pos_i = const.tile([P, NJ], I32, name="pos_i")
+            nc.gpsimd.iota(pos_i[:], pattern=[[1, NJ]], base=0, channel_multiplier=NJ)
+            pos_f = const.tile([P, NJ], F32, name="pos_f")
+            nc.vector.tensor_copy(out=pos_f[:], in_=pos_i[:])
+            for i in range(16):
+                scaled(ang[:, :, i], pos_f[:], BASE ** (-i / 16.0), 0.0)
+            scaled(turn[:], ang[:], 1.0 / two_pi, 0.0)
+
+        def rope_reduce():
+            turn_i = const.tile([P, NJ, 16], I32, name="turn_i")
+            nc.vector.tensor_copy(out=turn_i[:], in_=turn[:])
+            turn_f = small("turn_f")
+            nc.vector.tensor_copy(out=turn_f[:], in_=turn_i[:])
+            back = small("back")
+            scaled(back[:], turn_f[:], -two_pi, 0.0)
+            red = small("red")
+            nc.vector.tensor_tensor(out=red[:], in0=back[:], in1=ang[:], op=ALU.add)
+            over = small("over")
+            nc.vector.tensor_scalar(out=over[:], in0=red[:], scalar1=math.pi, scalar2=-two_pi, op0=ALU.is_gt,
+                                    op1=ALU.mult)
+            nc.vector.tensor_tensor(out=red2[:], in0=red[:], in1=over[:], op=ALU.add)
+
+        def rope_tables():
+            s2 = small("s2")
+            nc.scalar.activation(out=s2[:], in_=red2[:], func=ACT.Sin, scale=0.5)
+            s4 = small("s4")
+            nc.scalar.activation(out=s4[:], in_=red2[:], func=ACT.Sin, scale=0.25)
+            s4q = small("s4q")
+            nc.vector.tensor_tensor(out=s4q[:], in0=s4[:], in1=s4[:], op=ALU.mult)
+            s2q = small("s2q")
+            nc.vector.tensor_tensor(out=s2q[:], in0=s2[:], in1=s2[:], op=ALU.mult)
+            c2 = small("c2")
+            scaled(c2[:], s4q[:], -2.0, 1.0)
+            cosv = small("cosv")
+            scaled(cosv[:], s2q[:], -2.0, 1.0)
+            s2d = small("s2d")
+            scaled(s2d[:], s2[:], 2.0, 0.0)
+            sinv = small("sinv")
+            nc.vector.tensor_tensor(out=sinv[:], in0=s2d[:], in1=c2[:], op=ALU.mult)
+            for tab, val in ((cosf, cosv), (sinf, sinv)):
+                for half in range(2):
+                    scaled(tab[:, 0, 0:NJ, 16 * half:16 * half + 16], val[:], 1.0, 0.0)
+                scaled(tab[:, 0, NJ:2 * NJ, :], tab[:, 0, 0:NJ, :], 1.0, 0.0)
+                scaled(tab[:, 1, :, :], tab[:, 0, :, :], 1.0, 0.0)
+
+        res = {}
+        acc = {}
+
+        def mm(c, b):
+            width = PIECES[c][1]
+            xc, xs = xcodes[b]
+            wc, ws = wcodes[c]
+            for j in range(NJ):
+                bank = psum.tile([P, CW], F32, name="acc_%d_%d_%d" % (c, b, j), tag="bank")
+                acc[(c, b, j)] = bank
+                for g in range(NG):
+                    nc.tensor.matmul_mx(out=bank[:, 0:width], lhsT=xc[:, j, g * P:(g + 1) * P].bitcast(FP8X4),
+                                        lhsT_scale=xs[:, j, g * P:(g + 1) * P], rhs=wc[:, g, :].bitcast(FP8X4),
+                                        rhs_scale=ws[:, g, :], start=(g == 0), stop=(g == NG - 1))
+
+        def store(b, gb):
+            sc, blk = divmod(gb, 12)
+            nc.sync.dma_start(out=outs[gb % 3][b, gb // 3].rearrange("(p j) d -> p (j d)", j=NJ),
+                              in_=res[sc][:, b, blk, :, :].rearrange("p j d -> p (j d)"))
+
+        def evac(c, b):
+            col, width = PIECES[c]
+            nk = width // HD
+            sc, blk = divmod(col // HD, 12)
+            if sc not in res:
+                res[sc] = const.tile([P, NB, 12, NJ, HD], F32, name="res_%d" % sc)
+            rt = res[sc]
+            for j in range(NJ):
+                nc.vector.tensor_tensor(out=rt[:, b, blk:blk + nk, j, :],
+                                        in0=bias_bf[:, col:col + width].rearrange("p (k d) -> p k d", k=nk),
+                                        in1=acc[(c, b, j)][:, 0:width].rearrange("p (k d) -> p k d", k=nk),
+                                        op=ALU.add)
+            for k in range(nk):
+                if (col // HD + k) % 3 == 2:
+                    store(b, col // HD + k)
+
+        def rope(c, b0, b1):
+            col, width = PIECES[c]
+            gb0 = col // HD
+            nk = width // HD
+            sc = gb0 // 12
+            rv = res[sc][:].rearrange("p b k j d -> p b (k j) d")
+            runs = []
+            for k in range(nk):
+                if (gb0 + k) % 3 == 2:
+                    continue
+                if runs and runs[-1][1] == gb0 + k:
+                    runs[-1][1] = gb0 + k + 1
+                else:
+                    runs.append([gb0 + k, gb0 + k + 1])
+            nb = b1 - b0
+            for k0, k1 in runs:
+                on_vector = c in ROPE_ON_VECTOR or (c in SMALL_ON_VECTOR and k1 - k0 == 1)
+                eng = nc.vector if on_vector else nc.gpsimd
+                rows = NJ * (k1 - k0)
+                r0 = NJ * (k0 - 12 * sc)
+                u = scr.tile([P, NB, 2 * NJ, 32], F32, name="u_%d_%d_%d" % (c, b0, k0), tag="u")
+                v = scr.tile([P, NB, 2 * NJ, 32], F32, name="v_%d_%d_%d" % (c, b0, k0), tag="v")
+                x = rv[:, b0:b1, r0:r0 + rows, 0:32]
+                eng.tensor_tensor(out=u[:, 0:nb, 0:rows, :], in0=x, in1=cosf[:, 0:nb, 0:rows, :], op=ALU.mult)
+                eng.tensor_tensor(out=v[:, 0:nb, 0:rows, :], in0=x, in1=sinf[:, 0:nb, 0:rows, :], op=ALU.mult)
+                eng.tensor_tensor(out=rv[:, b0:b1, r0:r0 + rows, 0:16], in0=u[:, 0:nb, 0:rows, 0:16],
+                                  in1=v[:, 0:nb, 0:rows, 16:32], op=ALU.subtract)
+                eng.tensor_tensor(out=rv[:, b0:b1, r0:r0 + rows, 16:32], in0=u[:, 0:nb, 0:rows, 16:32],
+                                  in1=v[:, 0:nb, 0:rows, 0:16], op=ALU.add)
+                for b in range(b0, b1):
+                    for gb in range(k0, k1):
+                        store(b, gb)
+
+        rope_angles()
+        widen(0, (1,))
+        for j in range(NJ):
+            x_transpose(0, j)
+        interleave(0, (0, 1))
+        rope_reduce()
+        for j in range(NJ):
+            x_evac(0, j)
+        interleave(0, (1, 2))
+        quant(0, (0, 1))
+        x_quant(0, 0)
+        quant(0, (1, 2))
+        x_quant(0, 2)
+        widen(1, ())
+        rope_tables()
+        for j in range(NJ):
+            x_transpose(1, j)
+        for j in range(NJ):
+            x_evac(1, j)
+        x_quant(1, 0)
+        x_quant(1, 2)
+
+        for c in range(NP):
+            if c + 2 < NP:
+                widen(c + 2, ())
+            mm(c, 0)
+            if c + 1 < NP:
+                interleave(c + 1, (0, 2))
+            evac(c, 0)
+            mm(c, 1)
+            if c + 1 < NP:
+                quant(c + 1, (0, 2))
+            evac(c, 1)
+            rope(c, 0, 2)

@@ -20,17 +20,17 @@ P = 128
 NB = 2
 NJ = 4
 NG = 2
-NC = 6
-CW = 512
 HD = 128
+HW = 384
+NCH = 4
+CHW = 768
 BASE = 10000.0
 
-PIECES = ((0, 512), (512, 512), (1024, 512), (1536, 512), (2048, 512), (2560, 256), (2816, 256))
+PIECES = ((0, 0), (0, 1), (1, 0), (1, 1), (2, 0), (2, 1), (3, 0), (3, 1))
 NP = len(PIECES)
-V_COLS = (512, 256, 160, 96, 64, 0, 0)
-ROPE_ON_VECTOR = (4, 5, 6)
-SMALL_ON_VECTOR = (0, 1, 2, 3, 4, 5, 6)
-BYTE_RANGES = ((0, 512), (512, 1024), (1024, 2048), (2048, 3072))
+INTER_ON_VECTOR = (0, 1, 2, 3)
+ROPE_ON_VECTOR = ()
+LAG = 2
 
 
 def tile_pgtattention_pa_kernel(tc, hidden_states, W_qkv_bytes, W_qkv_scale, b_qkv, out_0, out_1, out_2):
@@ -38,9 +38,11 @@ def tile_pgtattention_pa_kernel(tc, hidden_states, W_qkv_bytes, W_qkv_scale, b_q
     outs = (out_0, out_1, out_2)
 
     with ExitStack() as ctx:
+        ctx.enter_context(tc.manual_schedule())
         const = ctx.enter_context(tc.tile_pool(name="const", bufs=1))
         stage = ctx.enter_context(tc.tile_pool(name="stage", bufs=2))
         codes = ctx.enter_context(tc.tile_pool(name="codes", bufs=3))
+        resp = ctx.enter_context(tc.tile_pool(name="resp", bufs=3))
         scr = ctx.enter_context(tc.tile_pool(name="scr", bufs=2))
         psum = ctx.enter_context(tc.psum_pool(name="psum", bufs=8))
 
@@ -49,12 +51,11 @@ def tile_pgtattention_pa_kernel(tc, hidden_states, W_qkv_bytes, W_qkv_scale, b_q
         wview = W_qkv_bytes.rearrange("(g p t) n -> g p t n", g=NG, p=P, t=4)
         wbytes = {}
 
-        def load_bytes(r):
-            lo, hi = BYTE_RANGES[r]
+        def load_bytes(c):
             for g in range(NG):
-                wb = const.tile([P, 4, hi - lo], U8, name="wbytes_%d_%d" % (r, g))
-                nc.sync.dma_start(out=wb[:], in_=wview[g][:, :, lo:hi])
-                wbytes[(r, g)] = wb
+                wb = const.tile([P, 4, CHW], U8, name="wbytes_%d_%d" % (c, g))
+                nc.sync.dma_start(out=wb[:], in_=wview[g][:, :, c * CHW:(c + 1) * CHW])
+                wbytes[(c, g)] = wb
 
         xsb = {}
 
@@ -65,19 +66,18 @@ def tile_pgtattention_pa_kernel(tc, hidden_states, W_qkv_bytes, W_qkv_scale, b_q
                 nc.sync.dma_start(out=xt[:], in_=xv[:, j, :])
                 xsb[(b, j)] = xt
 
-        bias_bf = const.tile([P, NC * CW], BF16, name="bias_bf")
+        bias_bf = const.tile([P, NCH * CHW], BF16, name="bias_bf")
 
         def load_bias(lo, hi):
             nc.sync.dma_start(out=bias_bf[:, lo:hi], in_=b_qkv[lo:hi].partition_broadcast(P))
 
         load_bytes(0)
         load_x(0)
-        load_bias(0, CW)
-        load_bytes(1)
+        load_bias(0, CHW)
         load_x(1)
-        load_bias(CW, 2 * CW)
+        load_bytes(1)
         load_bytes(2)
-        load_bias(2 * CW, NC * CW)
+        load_bias(CHW, NCH * CHW)
         load_bytes(3)
 
         warm = const.tile([P, 1], F32, name="warm")
@@ -91,59 +91,49 @@ def tile_pgtattention_pa_kernel(tc, hidden_states, W_qkv_bytes, W_qkv_scale, b_q
         grp = {}
         wcodes = {}
 
-        def byte_plane(c, g, t):
-            col, width = PIECES[c]
-            for r in range(len(BYTE_RANGES)):
-                lo, hi = BYTE_RANGES[r]
-                if lo <= col < hi:
-                    return wbytes[(r, g)][:, t, col - lo:col + width - lo].bitcast(FP8)
-            return None
+        def widen(c, g, on_vector):
+            if c not in wide:
+                wide[c] = stage.tile([P, NG, 4, CHW], BF16, name="wide_%d" % c, tag="wide")
+            for t in range(4):
+                src = wbytes[(c, g)][:, t, :].bitcast(FP8)
+                if on_vector:
+                    nc.vector.tensor_scalar(out=wide[c][:, g, t, :], in0=src, scalar1=wsc[:, g, t:t + 1], scalar2=None,
+                                            op0=ALU.mult)
+                else:
+                    nc.scalar.activation(out=wide[c][:, g, t, :], in_=src, func=ACT.Copy, scale=wsc[:, g, t:t + 1])
 
-        def widen(c, on_vector):
-            width = PIECES[c][1]
-            wd = stage.tile([P, NG, 4, CW], BF16, name="wide_%d" % c, tag="wide")
-            wide[c] = wd
-            for g in range(NG):
-                for t in range(4):
-                    if g in on_vector:
-                        nc.vector.tensor_scalar(out=wd[:, g, t, 0:width], in0=byte_plane(c, g, t),
-                                                scalar1=wsc[:, g, t:t + 1], scalar2=None, op0=ALU.mult)
-                    else:
-                        nc.scalar.activation(out=wd[:, g, t, 0:width], in_=byte_plane(c, g, t), func=ACT.Copy,
-                                             scale=wsc[:, g, t:t + 1])
+        def width_of(i):
+            return 512 if PIECES[i][1] == 0 else 256
 
-        def interleave(c, gs):
-            width = PIECES[c][1]
-            wd = wide[c]
-            if c not in grp:
-                grp[c] = stage.tile([P, NG, width, 4], BF16, name="grp_%d" % c, tag="grp", align_bytes=64)
-            gr = grp[c]
-            g0, g1 = gs
-            a = V_COLS[c]
-            if a < width:
-                nc.scalar.copy(out=gr[:, g0:g1, a:width, :],
-                               in_=wd[:, g0:g1, :, a:width].rearrange("p g t n -> p g n t"))
-            if a > 0:
-                nc.vector.tensor_copy(out=gr[:, g0:g1, 0:a, :], in_=wd[:, g0:g1, :, 0:a].rearrange("p g t n -> p g n t"))
+        def interleave(i, g):
+            c, kind = PIECES[i]
+            width = width_of(i)
+            if i not in grp:
+                grp[i] = stage.tile([P, NG, width, 4], BF16, name="grp_%d" % i, tag="grp%d" % kind, align_bytes=64)
+            lo, hi = (0, 256) if kind == 0 else (256, HW)
+            src = wide[c][:, g, :, :].rearrange("p t (h x) -> p h x t", x=HW)[:, :, lo:hi, :]
+            dst = grp[i][:, g, :, :].rearrange("p (h n) t -> p h n t", h=2)
+            if i in INTER_ON_VECTOR:
+                nc.vector.tensor_copy(out=dst, in_=src)
+            else:
+                nc.scalar.copy(out=dst, in_=src)
 
-        def quant(c, gs):
-            width = PIECES[c][1]
-            if c not in wcodes:
-                wc = codes.tile([P, NG, width], U32, name="wc_%d" % c, tag="wc", align_bytes=64)
-                ws = codes.tile([P, NG, width], U8, name="ws_%d" % c, tag="ws", align_bytes=64)
-                wcodes[c] = (wc, ws)
-            wc, ws = wcodes[c]
-            g0, g1 = gs
-            nc.vector.quantize_mx(out=wc[:, g0:g1, :].rearrange("p g n -> p (g n)").bitcast(FP8X4),
-                                  scales=ws[:, g0:g1, :].rearrange("p g n -> p (g n)"),
-                                  in_=grp[c][:, g0:g1, :, :].rearrange("p g n t -> p (g n t)"))
+        def quant(i):
+            width = width_of(i)
+            kind = PIECES[i][1]
+            wc = codes.tile([P, NG, width], U32, name="wc_%d" % i, tag="wc%d" % kind, align_bytes=64)
+            ws = codes.tile([P, NG, width], U8, name="ws_%d" % i, tag="ws%d" % kind, align_bytes=64)
+            wcodes[i] = (wc, ws)
+            nc.vector.quantize_mx(out=wc[:].rearrange("p g n -> p (g n)").bitcast(FP8X4),
+                                  scales=ws[:].rearrange("p g n -> p (g n)"),
+                                  in_=grp[i][:].rearrange("p g n t -> p (g n t)"))
 
         xbank = {}
         xgrp = {}
         xcodes = {}
 
         def x_transpose(b, j):
-            bank = psum.tile([P, CW], F32, name="xbank_%d_%d" % (b, j), tag="bank")
+            bank = psum.tile([P, 512], F32, name="xbank_%d_%d" % (b, j), tag="bank")
             xbank[(b, j)] = bank
             words = xsb[(b, j)][:].bitcast(F32)
             for g in range(NG):
@@ -167,15 +157,15 @@ def tile_pgtattention_pa_kernel(tc, hidden_states, W_qkv_bytes, W_qkv_scale, b_q
                                   scales=xs[:, j0:j0 + 2, :].rearrange("p j n -> p (j n)"),
                                   in_=xgrp[b][:, j0:j0 + 2, :].rearrange("p j n -> p (j n)"))
 
-        cosf = const.tile([P, NB, 2 * NJ, 32], F32, name="cosf")
-        sinf = const.tile([P, NB, 2 * NJ, 32], F32, name="sinf")
+        cosf = const.tile([P, 4, NJ, 32], F32, name="cosf")
+        sinf = const.tile([P, 4, NJ, 32], F32, name="sinf")
         two_pi = 2.0 * math.pi
 
         def small(name):
             return const.tile([P, NJ, 16], F32, name=name)
 
-        def scaled(dst, src, mul, add):
-            nc.vector.tensor_scalar(out=dst, in0=src, scalar1=mul, scalar2=add, op0=ALU.mult, op1=ALU.add)
+        def scaled(dst, src, mul, add, eng=None):
+            (eng or nc.vector).tensor_scalar(out=dst, in0=src, scalar1=mul, scalar2=add, op0=ALU.mult, op1=ALU.add)
 
         red2 = small("red2")
         ang = small("ang")
@@ -204,129 +194,161 @@ def tile_pgtattention_pa_kernel(tc, hidden_states, W_qkv_bytes, W_qkv_scale, b_q
                                     op1=ALU.mult)
             nc.vector.tensor_tensor(out=red2[:], in0=red[:], in1=over[:], op=ALU.add)
 
-        def rope_tables():
-            s2 = small("s2")
+        s2 = small("s2")
+        s4 = small("s4")
+
+        def rope_sines():
             nc.scalar.activation(out=s2[:], in_=red2[:], func=ACT.Sin, scale=0.5)
-            s4 = small("s4")
             nc.scalar.activation(out=s4[:], in_=red2[:], func=ACT.Sin, scale=0.25)
+
+        def rope_tables():
+            eng = nc.gpsimd
             s4q = small("s4q")
-            nc.vector.tensor_tensor(out=s4q[:], in0=s4[:], in1=s4[:], op=ALU.mult)
+            eng.tensor_tensor(out=s4q[:], in0=s4[:], in1=s4[:], op=ALU.mult)
             s2q = small("s2q")
-            nc.vector.tensor_tensor(out=s2q[:], in0=s2[:], in1=s2[:], op=ALU.mult)
+            eng.tensor_tensor(out=s2q[:], in0=s2[:], in1=s2[:], op=ALU.mult)
             c2 = small("c2")
-            scaled(c2[:], s4q[:], -2.0, 1.0)
+            scaled(c2[:], s4q[:], -2.0, 1.0, eng)
             cosv = small("cosv")
-            scaled(cosv[:], s2q[:], -2.0, 1.0)
+            scaled(cosv[:], s2q[:], -2.0, 1.0, eng)
             s2d = small("s2d")
-            scaled(s2d[:], s2[:], 2.0, 0.0)
+            scaled(s2d[:], s2[:], 2.0, 0.0, eng)
             sinv = small("sinv")
-            nc.vector.tensor_tensor(out=sinv[:], in0=s2d[:], in1=c2[:], op=ALU.mult)
+            eng.tensor_tensor(out=sinv[:], in0=s2d[:], in1=c2[:], op=ALU.mult)
             for tab, val in ((cosf, cosv), (sinf, sinv)):
                 for half in range(2):
-                    scaled(tab[:, 0, 0:NJ, 16 * half:16 * half + 16], val[:], 1.0, 0.0)
-                scaled(tab[:, 0, NJ:2 * NJ, :], tab[:, 0, 0:NJ, :], 1.0, 0.0)
-                scaled(tab[:, 1, :, :], tab[:, 0, :, :], 1.0, 0.0)
+                    scaled(tab[:, 0, :, 16 * half:16 * half + 16], val[:], 1.0, 0.0, eng)
+            for tab in (cosf, sinf):
+                scaled(tab[:, 1, :, :], tab[:, 0, :, :], 1.0, 0.0, eng)
+            for tab in (cosf, sinf):
+                scaled(tab[:, 2:4, :, :], tab[:, 0:2, :, :], 1.0, 0.0, eng)
 
         res = {}
         acc = {}
 
-        def mm(c, b):
-            width = PIECES[c][1]
+        def mm(i, b):
+            width = width_of(i)
+            per = 512 // width
             xc, xs = xcodes[b]
-            wc, ws = wcodes[c]
+            wc, ws = wcodes[i]
             for j in range(NJ):
-                bank = psum.tile([P, CW], F32, name="acc_%d_%d_%d" % (c, b, j), tag="bank")
-                acc[(c, b, j)] = bank
+                if j % per == 0:
+                    acc[(i, b, j // per)] = psum.tile([P, 512], F32, name="acc_%d_%d_%d" % (i, b, j), tag="bank")
+                bank = acc[(i, b, j // per)]
+                lo = (j % per) * width
                 for g in range(NG):
-                    nc.tensor.matmul_mx(out=bank[:, 0:width], lhsT=xc[:, j, g * P:(g + 1) * P].bitcast(FP8X4),
+                    nc.tensor.matmul_mx(out=bank[:, lo:lo + width], lhsT=xc[:, j, g * P:(g + 1) * P].bitcast(FP8X4),
                                         lhsT_scale=xs[:, j, g * P:(g + 1) * P], rhs=wc[:, g, :].bitcast(FP8X4),
                                         rhs_scale=ws[:, g, :], start=(g == 0), stop=(g == NG - 1))
 
-        def store(b, gb):
-            sc, blk = divmod(gb, 12)
-            nc.sync.dma_start(out=outs[gb % 3][b, gb // 3].rearrange("(p j) d -> p (j d)", j=NJ),
-                              in_=res[sc][:, b, blk, :, :].rearrange("p j d -> p (j d)"))
+        bias_heads = bias_bf[:].rearrange("p (h x) -> p h x", x=HW)
 
-        def evac(c, b):
-            col, width = PIECES[c]
-            nk = width // HD
-            sc, blk = divmod(col // HD, 12)
-            if sc not in res:
-                res[sc] = const.tile([P, NB, 12, NJ, HD], F32, name="res_%d" % sc)
-            rt = res[sc]
-            for j in range(NJ):
-                nc.vector.tensor_tensor(out=rt[:, b, blk:blk + nk, j, :],
-                                        in0=bias_bf[:, col:col + width].rearrange("p (k d) -> p k d", k=nk),
-                                        in1=acc[(c, b, j)][:, 0:width].rearrange("p (k d) -> p k d", k=nk),
-                                        op=ALU.add)
-            for k in range(nk):
-                if (col // HD + k) % 3 == 2:
-                    store(b, col // HD + k)
+        def store(i, b, k):
+            c, kind = PIECES[i]
+            if kind == 0:
+                head, part = 2 * c + k // 2, k % 2
+            else:
+                head, part = 2 * c + k, 2
+            nc.sync.dma_start(out=outs[part][b, head].rearrange("(p j) d -> p (j d)", j=NJ),
+                              in_=res[i][:, k, b, :, :].rearrange("p j d -> p (j d)"))
 
-        def rope(c, b0, b1):
-            col, width = PIECES[c]
-            gb0 = col // HD
-            nk = width // HD
-            sc = gb0 // 12
-            rv = res[sc][:].rearrange("p b k j d -> p b (k j) d")
-            runs = []
-            for k in range(nk):
-                if (gb0 + k) % 3 == 2:
-                    continue
-                if runs and runs[-1][1] == gb0 + k:
-                    runs[-1][1] = gb0 + k + 1
-                else:
-                    runs.append([gb0 + k, gb0 + k + 1])
-            nb = b1 - b0
-            for k0, k1 in runs:
-                on_vector = c in ROPE_ON_VECTOR or (c in SMALL_ON_VECTOR and k1 - k0 == 1)
-                eng = nc.vector if on_vector else nc.gpsimd
-                rows = NJ * (k1 - k0)
-                r0 = NJ * (k0 - 12 * sc)
-                u = scr.tile([P, NB, 2 * NJ, 32], F32, name="u_%d_%d_%d" % (c, b0, k0), tag="u")
-                v = scr.tile([P, NB, 2 * NJ, 32], F32, name="v_%d_%d_%d" % (c, b0, k0), tag="v")
-                x = rv[:, b0:b1, r0:r0 + rows, 0:32]
-                eng.tensor_tensor(out=u[:, 0:nb, 0:rows, :], in0=x, in1=cosf[:, 0:nb, 0:rows, :], op=ALU.mult)
-                eng.tensor_tensor(out=v[:, 0:nb, 0:rows, :], in0=x, in1=sinf[:, 0:nb, 0:rows, :], op=ALU.mult)
-                eng.tensor_tensor(out=rv[:, b0:b1, r0:r0 + rows, 0:16], in0=u[:, 0:nb, 0:rows, 0:16],
-                                  in1=v[:, 0:nb, 0:rows, 16:32], op=ALU.subtract)
-                eng.tensor_tensor(out=rv[:, b0:b1, r0:r0 + rows, 16:32], in0=u[:, 0:nb, 0:rows, 16:32],
-                                  in1=v[:, 0:nb, 0:rows, 0:16], op=ALU.add)
-                for b in range(b0, b1):
-                    for gb in range(k0, k1):
-                        store(b, gb)
+        def evac(i, b):
+            c, kind = PIECES[i]
+            nk = 4 if kind == 0 else 2
+            if i not in res:
+                res[i] = resp.tile([P, nk, NB, NJ, HD], F32, name="res_%d" % i, tag="res%d" % kind)
+            if kind == 0:
+                for j in range(NJ):
+                    nc.vector.tensor_tensor(out=res[i][:, :, b, j, :].rearrange("p (h q) d -> p h q d", h=2),
+                                            in0=bias_heads[:, 2 * c:2 * c + 2, 0:256].rearrange("p h (q d) -> p h q d", q=2),
+                                            in1=acc[(i, b, j)][:].rearrange("p (h q d) -> p h q d", h=2, q=2),
+                                            op=ALU.add)
+            else:
+                for jj in range(NJ // 2):
+                    nc.vector.tensor_tensor(out=res[i][:, :, b, 2 * jj:2 * jj + 2, :].rearrange("p h j d -> p j h d"),
+                                            in0=bias_heads[:, 2 * c:2 * c + 2, 256:HW].unsqueeze(1).to_broadcast([P, 2, 2, HD]),
+                                            in1=acc[(i, b, jj)][:].rearrange("p (j h d) -> p j h d", j=2, h=2),
+                                            op=ALU.add)
+
+        def stores(i, b):
+            for k in range(4 if PIECES[i][1] == 0 else 2):
+                store(i, b, k)
+
+        def rope(i, b, k0=0, k1=4, eng=None):
+            eng = eng or nc.gpsimd
+            n = k1 - k0
+            u = scr.tile([P, 4, NJ, 32], F32, name="u_%d_%d_%d" % (i, b, k0), tag="u")
+            v = scr.tile([P, 4, NJ, 32], F32, name="v_%d_%d_%d" % (i, b, k0), tag="v")
+            x = res[i][:, k0:k1, b, :, 0:32]
+            eng.tensor_tensor(out=u[:, 0:n], in0=x, in1=cosf[:, 0:n], op=ALU.mult)
+            eng.tensor_tensor(out=v[:, 0:n], in0=x, in1=sinf[:, 0:n], op=ALU.mult)
+            eng.tensor_tensor(out=res[i][:, k0:k1, b, :, 0:16], in0=u[:, 0:n, :, 0:16], in1=v[:, 0:n, :, 16:32], op=ALU.subtract)
+            eng.tensor_tensor(out=res[i][:, k0:k1, b, :, 16:32], in0=u[:, 0:n, :, 16:32], in1=v[:, 0:n, :, 0:16], op=ALU.add)
 
         rope_angles()
-        widen(0, (1,))
+        rope_reduce()
+        rope_sines()
+        rope_tables()
+        widen(0, 0, True)
+        widen(0, 1, False)
         for j in range(NJ):
             x_transpose(0, j)
-        interleave(0, (0, 1))
-        rope_reduce()
+        interleave(0, 0)
         for j in range(NJ):
             x_evac(0, j)
-        interleave(0, (1, 2))
-        quant(0, (0, 1))
+        interleave(0, 1)
+        quant(0)
         x_quant(0, 0)
-        quant(0, (1, 2))
         x_quant(0, 2)
-        widen(1, ())
-        rope_tables()
         for j in range(NJ):
             x_transpose(1, j)
         for j in range(NJ):
             x_evac(1, j)
+        mm(0, 0)
+        interleave(1, 0)
+        interleave(1, 1)
+        quant(1)
         x_quant(1, 0)
         x_quant(1, 2)
+        mm(0, 1)
+        widened = [0]
 
-        for c in range(NP):
-            if c + 2 < NP:
-                widen(c + 2, ())
-            mm(c, 0)
-            if c + 1 < NP:
-                interleave(c + 1, (0, 2))
-            evac(c, 0)
-            mm(c, 1)
-            if c + 1 < NP:
-                quant(c + 1, (0, 2))
-            evac(c, 1)
-            rope(c, 0, 2)
+        def prepare(i):
+            c = PIECES[i][0]
+            if c not in widened:
+                widen(c, 0, False)
+                widen(c, 1, False)
+                widened.append(c)
+            interleave(i, 0)
+            interleave(i, 1)
+
+        pending = []
+
+        def flush(now):
+            while pending and pending[0][0] <= now:
+                t, i, b = pending.pop(0)
+                stores(i, b)
+
+        step = 0
+        for i in range(NP):
+            for b in range(NB):
+                evac(i, b)
+                if PIECES[i][1] == 0:
+                    if (i, b) in ROPE_ON_VECTOR:
+                        rope(i, b, 0, 4, nc.vector)
+                        stores(i, b)
+                    else:
+                        rope(i, b)
+                        pending.append((step + LAG, i, b))
+                else:
+                    stores(i, b)
+                flush(step)
+                step += 1
+                if b == 0 and i + 1 < NP:
+                    mm(i + 1, 0)
+            if i + 1 < NP:
+                mm(i + 1, 1)
+            if i + 2 < NP:
+                prepare(i + 2)
+                quant(i + 2)
+        flush(step + LAG)

@@ -22,15 +22,17 @@ NJ = 4
 NG = 2
 HD = 128
 HW = 384
-NCH = 4
-CHW = 768
+NH = 8
 BASE = 10000.0
 
-PIECES = ((0, 0), (0, 1), (1, 0), (1, 1), (2, 0), (2, 1), (3, 0), (3, 1))
+CHUNKS = ((0, 2), (2, 2), (4, 2), (6, 1), (7, 1))
+NCH = len(CHUNKS)
+PIECES = tuple((c, kind) for c in range(NCH) for kind in range(2))
+LAGS = (2, 3)
 NP = len(PIECES)
-INTER_ON_VECTOR = (0, 1, 2, 3)
-ROPE_ON_VECTOR = ()
-LAG = 2
+INTER_ON_VECTOR = ((0, 0), (0, 1), (1, 0), (1, 1), (2, 0), (2, 1), (3, 0), (3, 1))
+ROPE_ON_VECTOR = ((8, 0), (8, 1))
+SPLIT = ()
 
 
 def tile_pgtattention_pa_kernel(tc, hidden_states, W_qkv_bytes, W_qkv_scale, b_qkv, out_0, out_1, out_2):
@@ -51,11 +53,18 @@ def tile_pgtattention_pa_kernel(tc, hidden_states, W_qkv_bytes, W_qkv_scale, b_q
         wview = W_qkv_bytes.rearrange("(g p t) n -> g p t n", g=NG, p=P, t=4)
         wbytes = {}
 
-        def load_bytes(c):
+        def load_bytes(c, by_plane=False):
+            h0, nh = CHUNKS[c]
+            lo, hi = h0 * HW, (h0 + nh) * HW
             for g in range(NG):
-                wb = const.tile([P, 4, CHW], U8, name="wbytes_%d_%d" % (c, g))
-                nc.sync.dma_start(out=wb[:], in_=wview[g][:, :, c * CHW:(c + 1) * CHW])
-                wbytes[(c, g)] = wb
+                wbytes[(c, g)] = const.tile([P, 4, hi - lo], U8, name="wbytes_%d_%d" % (c, g))
+            if by_plane:
+                for t in range(4):
+                    for g in range(NG):
+                        nc.sync.dma_start(out=wbytes[(c, g)][:, t, :], in_=wview[g][:, t, lo:hi])
+            else:
+                for g in range(NG):
+                    nc.sync.dma_start(out=wbytes[(c, g)][:], in_=wview[g][:, :, lo:hi])
 
         xsb = {}
 
@@ -66,19 +75,20 @@ def tile_pgtattention_pa_kernel(tc, hidden_states, W_qkv_bytes, W_qkv_scale, b_q
                 nc.sync.dma_start(out=xt[:], in_=xv[:, j, :])
                 xsb[(b, j)] = xt
 
-        bias_bf = const.tile([P, NCH * CHW], BF16, name="bias_bf")
+        bias_bf = const.tile([P, NH * HW], BF16, name="bias_bf")
 
         def load_bias(lo, hi):
             nc.sync.dma_start(out=bias_bf[:, lo:hi], in_=b_qkv[lo:hi].partition_broadcast(P))
 
-        load_bytes(0)
+        load_bytes(0, True)
         load_x(0)
-        load_bias(0, CHW)
+        load_bias(0, 2 * HW)
         load_x(1)
         load_bytes(1)
         load_bytes(2)
-        load_bias(CHW, NCH * CHW)
-        load_bytes(3)
+        load_bias(2 * HW, NH * HW)
+        for c in range(3, NCH):
+            load_bytes(c)
 
         warm = const.tile([P, 1], F32, name="warm")
         nc.vector.memset(warm[:], 0.0)
@@ -91,10 +101,10 @@ def tile_pgtattention_pa_kernel(tc, hidden_states, W_qkv_bytes, W_qkv_scale, b_q
         grp = {}
         wcodes = {}
 
-        def widen(c, g, on_vector):
+        def widen(c, g, on_vector, planes=(0, 1, 2, 3)):
             if c not in wide:
-                wide[c] = stage.tile([P, NG, 4, CHW], BF16, name="wide_%d" % c, tag="wide")
-            for t in range(4):
+                wide[c] = stage.tile([P, NG, 4, CHUNKS[c][1] * HW], BF16, name="wide_%d" % c, tag="wide")
+            for t in planes:
                 src = wbytes[(c, g)][:, t, :].bitcast(FP8)
                 if on_vector:
                     nc.vector.tensor_scalar(out=wide[c][:, g, t, :], in0=src, scalar1=wsc[:, g, t:t + 1], scalar2=None,
@@ -102,8 +112,12 @@ def tile_pgtattention_pa_kernel(tc, hidden_states, W_qkv_bytes, W_qkv_scale, b_q
                 else:
                     nc.scalar.activation(out=wide[c][:, g, t, :], in_=src, func=ACT.Copy, scale=wsc[:, g, t:t + 1])
 
+        def blocks_of(i):
+            c, kind = PIECES[i]
+            return CHUNKS[c][1] * (2 - kind)
+
         def width_of(i):
-            return 512 if PIECES[i][1] == 0 else 256
+            return HD * blocks_of(i)
 
         def interleave(i, g):
             c, kind = PIECES[i]
@@ -112,8 +126,8 @@ def tile_pgtattention_pa_kernel(tc, hidden_states, W_qkv_bytes, W_qkv_scale, b_q
                 grp[i] = stage.tile([P, NG, width, 4], BF16, name="grp_%d" % i, tag="grp%d" % kind, align_bytes=64)
             lo, hi = (0, 256) if kind == 0 else (256, HW)
             src = wide[c][:, g, :, :].rearrange("p t (h x) -> p h x t", x=HW)[:, :, lo:hi, :]
-            dst = grp[i][:, g, :, :].rearrange("p (h n) t -> p h n t", h=2)
-            if i in INTER_ON_VECTOR:
+            dst = grp[i][:, g, :, :].rearrange("p (h n) t -> p h n t", h=CHUNKS[c][1])
+            if (i, g) in INTER_ON_VECTOR:
                 nc.vector.tensor_copy(out=dst, in_=src)
             else:
                 nc.scalar.copy(out=dst, in_=src)
@@ -171,28 +185,34 @@ def tile_pgtattention_pa_kernel(tc, hidden_states, W_qkv_bytes, W_qkv_scale, b_q
         ang = small("ang")
         turn = small("turn")
 
-        def rope_angles():
-            pos_i = const.tile([P, NJ], I32, name="pos_i")
-            nc.gpsimd.iota(pos_i[:], pattern=[[1, NJ]], base=0, channel_multiplier=NJ)
-            pos_f = const.tile([P, NJ], F32, name="pos_f")
-            nc.vector.tensor_copy(out=pos_f[:], in_=pos_i[:])
-            for i in range(16):
-                scaled(ang[:, :, i], pos_f[:], BASE ** (-i / 16.0), 0.0)
-            scaled(turn[:], ang[:], 1.0 / two_pi, 0.0)
+        pos_f = const.tile([P, NJ], F32, name="pos_f")
+        turn_i = const.tile([P, NJ, 16], I32, name="turn_i")
+        turn_f = small("turn_f")
+        back = small("back")
+        red = small("red")
+        over = small("over")
 
-        def rope_reduce():
-            turn_i = const.tile([P, NJ, 16], I32, name="turn_i")
-            nc.vector.tensor_copy(out=turn_i[:], in_=turn[:])
-            turn_f = small("turn_f")
-            nc.vector.tensor_copy(out=turn_f[:], in_=turn_i[:])
-            back = small("back")
-            scaled(back[:], turn_f[:], -two_pi, 0.0)
-            red = small("red")
-            nc.vector.tensor_tensor(out=red[:], in0=back[:], in1=ang[:], op=ALU.add)
-            over = small("over")
-            nc.vector.tensor_scalar(out=over[:], in0=red[:], scalar1=math.pi, scalar2=-two_pi, op0=ALU.is_gt,
-                                    op1=ALU.mult)
-            nc.vector.tensor_tensor(out=red2[:], in0=red[:], in1=over[:], op=ALU.add)
+        def angle_step(n):
+            if n == 0:
+                scaled(ang[:, :, 0], pos_f[:], 1.0, 0.0)
+            elif n <= 4:
+                w = 2 ** (n - 1)
+                scaled(ang[:, :, w:2 * w], ang[:, :, 0:w], BASE ** (-w / 16.0), 0.0)
+            elif n == 5:
+                scaled(turn[:], ang[:], 1.0 / two_pi, 0.0)
+            elif n == 6:
+                nc.vector.tensor_copy(out=turn_i[:], in_=turn[:])
+            elif n == 7:
+                nc.vector.tensor_copy(out=turn_f[:], in_=turn_i[:])
+            elif n == 8:
+                scaled(back[:], turn_f[:], -two_pi, 0.0)
+            elif n == 9:
+                nc.vector.tensor_tensor(out=red[:], in0=back[:], in1=ang[:], op=ALU.add)
+            elif n == 10:
+                nc.vector.tensor_scalar(out=over[:], in0=red[:], scalar1=math.pi, scalar2=-two_pi, op0=ALU.is_gt,
+                                        op1=ALU.mult)
+            else:
+                nc.vector.tensor_tensor(out=red2[:], in0=red[:], in1=over[:], op=ALU.add)
 
         s2 = small("s2")
         s4 = small("s4")
@@ -245,52 +265,66 @@ def tile_pgtattention_pa_kernel(tc, hidden_states, W_qkv_bytes, W_qkv_scale, b_q
 
         def store(i, b, k):
             c, kind = PIECES[i]
+            h0 = CHUNKS[c][0]
             if kind == 0:
-                head, part = 2 * c + k // 2, k % 2
+                head, part = h0 + k // 2, k % 2
             else:
-                head, part = 2 * c + k, 2
+                head, part = h0 + k, 2
             nc.sync.dma_start(out=outs[part][b, head].rearrange("(p j) d -> p (j d)", j=NJ),
                               in_=res[i][:, k, b, :, :].rearrange("p j d -> p (j d)"))
 
         def evac(i, b):
             c, kind = PIECES[i]
-            nk = 4 if kind == 0 else 2
+            h0, nh = CHUNKS[c]
+            nk = blocks_of(i)
+            per = 4 // nk
             if i not in res:
                 res[i] = resp.tile([P, nk, NB, NJ, HD], F32, name="res_%d" % i, tag="res%d" % kind)
-            if kind == 0:
+            if per == 1:
                 for j in range(NJ):
                     nc.vector.tensor_tensor(out=res[i][:, :, b, j, :].rearrange("p (h q) d -> p h q d", h=2),
-                                            in0=bias_heads[:, 2 * c:2 * c + 2, 0:256].rearrange("p h (q d) -> p h q d", q=2),
+                                            in0=bias_heads[:, h0:h0 + 2, 0:256].rearrange("p h (q d) -> p h q d", q=2),
                                             in1=acc[(i, b, j)][:].rearrange("p (h q d) -> p h q d", h=2, q=2),
                                             op=ALU.add)
             else:
-                for jj in range(NJ // 2):
-                    nc.vector.tensor_tensor(out=res[i][:, :, b, 2 * jj:2 * jj + 2, :].rearrange("p h j d -> p j h d"),
-                                            in0=bias_heads[:, 2 * c:2 * c + 2, 256:HW].unsqueeze(1).to_broadcast([P, 2, 2, HD]),
-                                            in1=acc[(i, b, jj)][:].rearrange("p (j h d) -> p j h d", j=2, h=2),
+                if kind == 0:
+                    bias = bias_heads[:, h0, 0:256].rearrange("p (k d) -> p k d", k=nk)
+                else:
+                    bias = bias_heads[:, h0:h0 + nh, 256:HW]
+                for jj in range(NJ // per):
+                    nc.vector.tensor_tensor(out=res[i][:, :, b, per * jj:per * (jj + 1), :].rearrange("p k j d -> p j k d"),
+                                            in0=bias.unsqueeze(1).to_broadcast([P, per, nk, HD]),
+                                            in1=acc[(i, b, jj)][:].rearrange("p (j k d) -> p j k d", j=per, k=nk),
                                             op=ALU.add)
 
         def stores(i, b):
-            for k in range(4 if PIECES[i][1] == 0 else 2):
+            for k in range(blocks_of(i)):
                 store(i, b, k)
 
-        def rope(i, b, k0=0, k1=4, eng=None):
+        def rope(i, b, k0=0, k1=None, eng=None):
             eng = eng or nc.gpsimd
+            k1 = k1 or blocks_of(i)
             n = k1 - k0
-            u = scr.tile([P, 4, NJ, 32], F32, name="u_%d_%d_%d" % (i, b, k0), tag="u")
-            v = scr.tile([P, 4, NJ, 32], F32, name="v_%d_%d_%d" % (i, b, k0), tag="v")
+            own = "g" if eng is nc.gpsimd else "v"
+            u = scr.tile([P, n, NJ, 32], F32, name="u_%d_%d_%d" % (i, b, k0), tag="u" + own)
+            v = scr.tile([P, n, NJ, 32], F32, name="v_%d_%d_%d" % (i, b, k0), tag="v" + own)
             x = res[i][:, k0:k1, b, :, 0:32]
             eng.tensor_tensor(out=u[:, 0:n], in0=x, in1=cosf[:, 0:n], op=ALU.mult)
             eng.tensor_tensor(out=v[:, 0:n], in0=x, in1=sinf[:, 0:n], op=ALU.mult)
             eng.tensor_tensor(out=res[i][:, k0:k1, b, :, 0:16], in0=u[:, 0:n, :, 0:16], in1=v[:, 0:n, :, 16:32], op=ALU.subtract)
             eng.tensor_tensor(out=res[i][:, k0:k1, b, :, 16:32], in0=u[:, 0:n, :, 16:32], in1=v[:, 0:n, :, 0:16], op=ALU.add)
 
-        rope_angles()
-        rope_reduce()
+        pos_i = const.tile([P, NJ], I32, name="pos_i")
+        nc.gpsimd.iota(pos_i[:], pattern=[[1, NJ]], base=0, channel_multiplier=NJ)
+        nc.vector.tensor_copy(out=pos_f[:], in_=pos_i[:])
+        for n in range(8):
+            angle_step(n)
+        for t in range(4):
+            widen(0, 0, True, (t,))
+            angle_step(8 + t)
+        widen(0, 1, False)
         rope_sines()
         rope_tables()
-        widen(0, 0, True)
-        widen(0, 1, False)
         for j in range(NJ):
             x_transpose(0, j)
         interleave(0, 0)
@@ -325,9 +359,10 @@ def tile_pgtattention_pa_kernel(tc, hidden_states, W_qkv_bytes, W_qkv_scale, b_q
         pending = []
 
         def flush(now):
-            while pending and pending[0][0] <= now:
-                t, i, b = pending.pop(0)
-                stores(i, b)
+            for item in tuple(pending):
+                if item[0] <= now:
+                    stores(item[1], item[2])
+                    pending.remove(item)
 
         step = 0
         for i in range(NP):
@@ -335,12 +370,15 @@ def tile_pgtattention_pa_kernel(tc, hidden_states, W_qkv_bytes, W_qkv_scale, b_q
                 evac(i, b)
                 if PIECES[i][1] == 0:
                     if (i, b) in ROPE_ON_VECTOR:
-                        rope(i, b, 0, 4, nc.vector)
+                        rope(i, b, 0, None, nc.vector)
                         stores(i, b)
+                    elif (i, b) == SPLIT:
+                        rope(i, b, 0, blocks_of(i) // 2)
                     else:
                         rope(i, b)
-                        pending.append((step + LAG, i, b))
+                        pending.append((step + LAGS[b], i, b))
                 else:
+                    flush(step)
                     stores(i, b)
                 flush(step)
                 step += 1
@@ -351,4 +389,7 @@ def tile_pgtattention_pa_kernel(tc, hidden_states, W_qkv_bytes, W_qkv_scale, b_q
             if i + 2 < NP:
                 prepare(i + 2)
                 quant(i + 2)
-        flush(step + LAG)
+        flush(step + 9)
+        if SPLIT:
+            rope(SPLIT[0], SPLIT[1], blocks_of(SPLIT[0]) // 2, None, nc.vector)
+            stores(SPLIT[0], SPLIT[1])

@@ -125,12 +125,14 @@ def tile_pgtattention_pa_kernel(tc, hidden_states, W_qkv_bytes, W_qkv_scale, b_q
             if i not in grp:
                 grp[i] = stage.tile([P, NG, width, 4], BF16, name="grp_%d" % i, tag="grp%d" % kind, align_bytes=64)
             lo, hi = (0, 256) if kind == 0 else (256, HW)
-            src = wide[c][:, g, :, :].rearrange("p t (h x) -> p h x t", x=HW)[:, :, lo:hi, :]
-            dst = grp[i][:, g, :, :].rearrange("p (h n) t -> p h n t", h=CHUNKS[c][1])
-            if (i, g) in INTER_ON_VECTOR:
-                nc.vector.tensor_copy(out=dst, in_=src)
-            else:
-                nc.scalar.copy(out=dst, in_=src)
+            n = hi - lo
+            for h in range(CHUNKS[c][1]):
+                src = wide[c][:, g, :, h * HW + lo:h * HW + hi].rearrange("p t (c i) -> p c t i", i=4)
+                dst = grp[i][:, g, h * n:(h + 1) * n, :].rearrange("p (c i) t -> p c t i", i=4)
+                if (i, g) in INTER_ON_VECTOR:
+                    nc.vector.tensor_copy(out=dst, in_=src)
+                else:
+                    nc.scalar.copy(out=dst, in_=src)
 
         def quant(i):
             width = width_of(i)

@@ -28,11 +28,8 @@ BASE = 10000.0
 CHUNKS = ((0, 2), (2, 2), (4, 2), (6, 1), (7, 1))
 NCH = len(CHUNKS)
 PIECES = tuple((c, kind) for c in range(NCH) for kind in range(2))
-LAGS = (2, 3)
 NP = len(PIECES)
-INTER_ON_VECTOR = ((0, 0), (0, 1), (1, 0), (1, 1), (2, 0), (2, 1), (3, 0), (3, 1))
-ROPE_ON_VECTOR = ((8, 0), (8, 1))
-SPLIT = ()
+INTER_ON_VECTOR = ((0, 0), (0, 1), (1, 0), (1, 1), (2, 0), (2, 1))
 
 
 def tile_pgtattention_pa_kernel(tc, hidden_states, W_qkv_bytes, W_qkv_scale, b_qkv, out_0, out_1, out_2):
@@ -45,7 +42,7 @@ def tile_pgtattention_pa_kernel(tc, hidden_states, W_qkv_bytes, W_qkv_scale, b_q
         stage = ctx.enter_context(tc.tile_pool(name="stage", bufs=2))
         codes = ctx.enter_context(tc.tile_pool(name="codes", bufs=3))
         resp = ctx.enter_context(tc.tile_pool(name="resp", bufs=3))
-        scr = ctx.enter_context(tc.tile_pool(name="scr", bufs=2))
+        scr = ctx.enter_context(tc.tile_pool(name="scr", bufs=1))
         psum = ctx.enter_context(tc.psum_pool(name="psum", bufs=8))
 
         wsc = const.tile([P, NG, 4], F32, name="wsc")
@@ -173,8 +170,8 @@ def tile_pgtattention_pa_kernel(tc, hidden_states, W_qkv_bytes, W_qkv_scale, b_q
                                   scales=xs[:, j0:j0 + 2, :].rearrange("p j n -> p (j n)"),
                                   in_=xgrp[b][:, j0:j0 + 2, :].rearrange("p j n -> p (j n)"))
 
-        cosf = const.tile([P, 4, NJ, 32], F32, name="cosf")
-        sinf = const.tile([P, 4, NJ, 32], F32, name="sinf")
+        cosf = const.tile([P, NJ, 2, 16], F32, name="cosf")
+        sinf = const.tile([P, NJ, 2, 16], F32, name="sinf")
         two_pi = 2.0 * math.pi
 
         def small(name):
@@ -231,19 +228,12 @@ def tile_pgtattention_pa_kernel(tc, hidden_states, W_qkv_bytes, W_qkv_scale, b_q
             eng.tensor_tensor(out=s2q[:], in0=s2[:], in1=s2[:], op=ALU.mult)
             c2 = small("c2")
             scaled(c2[:], s4q[:], -2.0, 1.0, eng)
-            cosv = small("cosv")
-            scaled(cosv[:], s2q[:], -2.0, 1.0, eng)
             s2d = small("s2d")
             scaled(s2d[:], s2[:], 2.0, 0.0, eng)
-            sinv = small("sinv")
-            eng.tensor_tensor(out=sinv[:], in0=s2d[:], in1=c2[:], op=ALU.mult)
-            for tab, val in ((cosf, cosv), (sinf, sinv)):
-                for half in range(2):
-                    scaled(tab[:, 0, :, 16 * half:16 * half + 16], val[:], 1.0, 0.0, eng)
-            for tab in (cosf, sinf):
-                scaled(tab[:, 1, :, :], tab[:, 0, :, :], 1.0, 0.0, eng)
-            for tab in (cosf, sinf):
-                scaled(tab[:, 2:4, :, :], tab[:, 0:2, :, :], 1.0, 0.0, eng)
+            both = [P, NJ, 2, 16]
+            scaled(cosf[:], s2q[:].unsqueeze(2).to_broadcast(both), -2.0, 1.0, eng)
+            eng.tensor_tensor(out=sinf[:], in0=s2d[:].unsqueeze(2).to_broadcast(both), in1=c2[:].unsqueeze(2).to_broadcast(both),
+                              op=ALU.mult)
 
         res = {}
         acc = {}
@@ -303,18 +293,24 @@ def tile_pgtattention_pa_kernel(tc, hidden_states, W_qkv_bytes, W_qkv_scale, b_q
             for k in range(blocks_of(i)):
                 store(i, b, k)
 
-        def rope(i, b, k0=0, k1=None, eng=None):
-            eng = eng or nc.gpsimd
-            k1 = k1 or blocks_of(i)
-            n = k1 - k0
-            own = "g" if eng is nc.gpsimd else "v"
-            u = scr.tile([P, n, NJ, 32], F32, name="u_%d_%d_%d" % (i, b, k0), tag="u" + own)
-            v = scr.tile([P, n, NJ, 32], F32, name="v_%d_%d_%d" % (i, b, k0), tag="v" + own)
-            x = res[i][:, k0:k1, b, :, 0:32]
-            eng.tensor_tensor(out=u[:, 0:n], in0=x, in1=cosf[:, 0:n], op=ALU.mult)
-            eng.tensor_tensor(out=v[:, 0:n], in0=x, in1=sinf[:, 0:n], op=ALU.mult)
-            eng.tensor_tensor(out=res[i][:, k0:k1, b, :, 0:16], in0=u[:, 0:n, :, 0:16], in1=v[:, 0:n, :, 16:32], op=ALU.subtract)
-            eng.tensor_tensor(out=res[i][:, k0:k1, b, :, 16:32], in0=u[:, 0:n, :, 16:32], in1=v[:, 0:n, :, 0:16], op=ALU.add)
+        prod = {}
+
+        def rope_products(i, b, eng):
+            n = blocks_of(i)
+            u = scr.tile([P, n, NJ, 32], F32, name="u_%d_%d" % (i, b), tag="u%d" % b)
+            v = scr.tile([P, n, NJ, 32], F32, name="v_%d_%d" % (i, b), tag="v%d" % b)
+            prod[(i, b)] = (u, v)
+            x = res[i][:, :, b, :, 0:32]
+            shape = [P, n, NJ, 32]
+            eng.tensor_tensor(out=u[:], in0=x, in1=cosf[:].rearrange("p j h i -> p j (h i)").unsqueeze(1).to_broadcast(shape),
+                              op=ALU.mult)
+            eng.tensor_tensor(out=v[:], in0=x, in1=sinf[:].rearrange("p j h i -> p j (h i)").unsqueeze(1).to_broadcast(shape),
+                              op=ALU.mult)
+
+        def rope_sums(i, b, eng):
+            u, v = prod[(i, b)]
+            eng.tensor_tensor(out=res[i][:, :, b, :, 0:16], in0=u[:, :, :, 0:16], in1=v[:, :, :, 16:32], op=ALU.subtract)
+            eng.tensor_tensor(out=res[i][:, :, b, :, 16:32], in0=u[:, :, :, 16:32], in1=v[:, :, :, 0:16], op=ALU.add)
 
         pos_i = const.tile([P, NJ], I32, name="pos_i")
         nc.gpsimd.iota(pos_i[:], pattern=[[1, NJ]], base=0, channel_multiplier=NJ)
@@ -358,40 +354,32 @@ def tile_pgtattention_pa_kernel(tc, hidden_states, W_qkv_bytes, W_qkv_scale, b_q
             interleave(i, 0)
             interleave(i, 1)
 
-        pending = []
-
-        def flush(now):
-            for item in tuple(pending):
-                if item[0] <= now:
-                    stores(item[1], item[2])
-                    pending.remove(item)
-
-        step = 0
-        for i in range(NP):
-            for b in range(NB):
-                evac(i, b)
-                if PIECES[i][1] == 0:
-                    if (i, b) in ROPE_ON_VECTOR:
-                        rope(i, b, 0, None, nc.vector)
-                        stores(i, b)
-                    elif (i, b) == SPLIT:
-                        rope(i, b, 0, blocks_of(i) // 2)
-                    else:
-                        rope(i, b)
-                        pending.append((step + LAGS[b], i, b))
-                else:
-                    flush(step)
-                    stores(i, b)
-                flush(step)
-                step += 1
-                if b == 0 and i + 1 < NP:
-                    mm(i + 1, 0)
-            if i + 1 < NP:
-                mm(i + 1, 1)
-            if i + 2 < NP:
-                prepare(i + 2)
-                quant(i + 2)
-        flush(step + 9)
-        if SPLIT:
-            rope(SPLIT[0], SPLIT[1], blocks_of(SPLIT[0]) // 2, None, nc.vector)
-            stores(SPLIT[0], SPLIT[1])
+        for c in range(NCH):
+            qk, vv = 2 * c, 2 * c + 1
+            last = c == NCH - 1
+            evac(qk, 0)
+            if c > 0:
+                rope_sums(qk - 2, 1, nc.gpsimd)
+            rope_products(qk, 0, nc.gpsimd)
+            rope_sums(qk, 0, nc.gpsimd)
+            mm(vv, 0)
+            mm(vv, 1)
+            evac(qk, 1)
+            if c > 0:
+                stores(qk - 2, 1)
+            evac(vv, 0)
+            stores(vv, 0)
+            evac(vv, 1)
+            stores(vv, 1)
+            stores(qk, 0)
+            if not last:
+                prepare(qk + 2)
+                quant(qk + 2)
+                mm(qk + 2, 0)
+                mm(qk + 2, 1)
+                prepare(vv + 2)
+                quant(vv + 2)
+            rope_products(qk, 1, nc.vector)
+            if last:
+                rope_sums(qk, 1, nc.vector)
+                stores(qk, 1)

@@ -94,6 +94,15 @@ def tile_pgtattention_pa_kernel(tc, hidden_states, W_qkv_bytes, W_qkv_scale, b_q
         ident = const.tile([P, P], F32, name="ident")
         make_identity(nc, ident[:])
 
+        def keep_warm(banks, each):
+            for k in range(banks):
+                idle = psum.tile([P, 512], F32, name="idle_%d" % len(idles), tag="bank")
+                idles.append(idle)
+                for n in range(each):
+                    nc.tensor.matmul(out=idle[:, 0:P], lhsT=ident[:], rhs=ident[:], start=True, stop=True)
+
+        idles = []
+
         wide = {}
         grp = {}
         wcodes = {}
@@ -323,6 +332,7 @@ def tile_pgtattention_pa_kernel(tc, hidden_states, W_qkv_bytes, W_qkv_scale, b_q
         widen(0, 1, False)
         rope_sines()
         rope_tables()
+        keep_warm(1, 16)
         for j in range(NJ):
             x_transpose(0, j)
         interleave(0, 0)
@@ -332,6 +342,7 @@ def tile_pgtattention_pa_kernel(tc, hidden_states, W_qkv_bytes, W_qkv_scale, b_q
         quant(0)
         x_quant(0, 0)
         x_quant(0, 2)
+        keep_warm(1, 4)
         for j in range(NJ):
             x_transpose(1, j)
         for j in range(NJ):
@@ -364,6 +375,8 @@ def tile_pgtattention_pa_kernel(tc, hidden_states, W_qkv_bytes, W_qkv_scale, b_q
             rope_sums(qk, 0, nc.gpsimd)
             mm(vv, 0)
             mm(vv, 1)
+            if not last:
+                keep_warm(4 * CHUNKS[c][1], 1)
             evac(qk, 1)
             if c > 0:
                 stores(qk - 2, 1)

@@ -133,8 +133,8 @@ def tile_pgtattention_pa_kernel(tc, hidden_states, W_qkv_bytes, W_qkv_scale, b_q
             lo, hi = (0, 256) if kind == 0 else (256, HW)
             n = hi - lo
             for h in range(CHUNKS[c][1]):
-                src = wide[c][:, g, :, h * HW + lo:h * HW + hi].rearrange("p t (c i) -> p c t i", i=4)
-                dst = grp[i][:, g, h * n:(h + 1) * n, :].rearrange("p (c i) t -> p c t i", i=4)
+                src = wide[c][:, g, :, h * HW + lo:h * HW + hi].rearrange("p t (c i) -> p c t i", i=8)
+                dst = grp[i][:, g, h * n:(h + 1) * n, :].rearrange("p (c i) t -> p c t i", i=8)
                 if (i, g) in INTER_ON_VECTOR:
                     nc.vector.tensor_copy(out=dst, in_=src)
                 else:

@@ -30,6 +30,7 @@ NCH = len(CHUNKS)
 PIECES = tuple((c, kind) for c in range(NCH) for kind in range(2))
 NP = len(PIECES)
 INTER_ON_VECTOR = ((0, 0), (0, 1), (1, 0), (1, 1), (2, 0), (2, 1))
+INTER_ON_GPSIMD = ((2, 0, 0),)
 
 
 def tile_pgtattention_pa_kernel(tc, hidden_states, W_qkv_bytes, W_qkv_scale, b_qkv, out_0, out_1, out_2):
@@ -125,7 +126,7 @@ def tile_pgtattention_pa_kernel(tc, hidden_states, W_qkv_bytes, W_qkv_scale, b_q
         def width_of(i):
             return HD * blocks_of(i)
 
-        def interleave(i, g):
+        def interleave(i, g, early=False):
             c, kind = PIECES[i]
             width = width_of(i)
             if i not in grp:
@@ -135,7 +136,13 @@ def tile_pgtattention_pa_kernel(tc, hidden_states, W_qkv_bytes, W_qkv_scale, b_q
             for h in range(CHUNKS[c][1]):
                 src = wide[c][:, g, :, h * HW + lo:h * HW + hi].rearrange("p t (c i) -> p c t i", i=8)
                 dst = grp[i][:, g, h * n:(h + 1) * n, :].rearrange("p (c i) t -> p c t i", i=8)
-                if (i, g) in INTER_ON_VECTOR:
+                if (i, g, h) in INTER_ON_GPSIMD:
+                    if not early:
+                        continue
+                    nc.gpsimd.tensor_scalar(out=dst, in0=src, scalar1=1.0, scalar2=0.0, op0=ALU.mult, op1=ALU.add)
+                elif early:
+                    continue
+                elif (i, g) in INTER_ON_VECTOR:
                     nc.vector.tensor_copy(out=dst, in_=src)
                 else:
                     nc.scalar.copy(out=dst, in_=src)
@@ -354,7 +361,10 @@ def tile_pgtattention_pa_kernel(tc, hidden_states, W_qkv_bytes, W_qkv_scale, b_q
         x_quant(1, 0)
         x_quant(1, 2)
         mm(0, 1)
-        widened = [0]
+        widen(1, 0, False)
+        interleave(2, 0, True)
+        widen(1, 1, False)
+        widened = [0, 1]
 
         def prepare(i):
             c = PIECES[i][0]

@@ -30,7 +30,7 @@ NCH = len(CHUNKS)
 PIECES = tuple((c, kind) for c in range(NCH) for kind in range(2))
 NP = len(PIECES)
 INTER_ON_VECTOR = ((0, 0), (0, 1), (1, 0), (1, 1), (2, 0), (2, 1))
-INTER_ON_GPSIMD = ((2, 0, 0),)
+INTER_ON_GPSIMD = ((2, 0, 0), (3, 0, 0))
 
 
 def tile_pgtattention_pa_kernel(tc, hidden_states, W_qkv_bytes, W_qkv_scale, b_qkv, out_0, out_1, out_2):
@@ -363,6 +363,7 @@ def tile_pgtattention_pa_kernel(tc, hidden_states, W_qkv_bytes, W_qkv_scale, b_q
         mm(0, 1)
         widen(1, 0, False)
         interleave(2, 0, True)
+        interleave(3, 0, True)
         widen(1, 1, False)
         widened = [0, 1]
 

@@ -51,14 +51,18 @@ def tile_pgtattention_pa_kernel(tc, hidden_states, W_qkv_bytes, W_qkv_scale, b_q
         wview = W_qkv_bytes.rearrange("(g p t) n -> g p t n", g=NG, p=P, t=4)
         wbytes = {}
 
-        def load_bytes(c, by_plane=False):
+        def load_bytes(c, by_plane=0):
             h0, nh = CHUNKS[c]
             lo, hi = h0 * HW, (h0 + nh) * HW
             for g in range(NG):
                 wbytes[(c, g)] = const.tile([P, 4, hi - lo], U8, name="wbytes_%d_%d" % (c, g))
-            if by_plane:
+            if by_plane == 1:
                 for t in range(4):
                     for g in range(NG):
+                        nc.sync.dma_start(out=wbytes[(c, g)][:, t, :], in_=wview[g][:, t, lo:hi])
+            elif by_plane == 2:
+                for g in range(NG):
+                    for t in range(4):
                         nc.sync.dma_start(out=wbytes[(c, g)][:, t, :], in_=wview[g][:, t, lo:hi])
             else:
                 for g in range(NG):
@@ -78,11 +82,11 @@ def tile_pgtattention_pa_kernel(tc, hidden_states, W_qkv_bytes, W_qkv_scale, b_q
         def load_bias(lo, hi):
             nc.sync.dma_start(out=bias_bf[:, lo:hi], in_=b_qkv[lo:hi].partition_broadcast(P))
 
-        load_bytes(0, True)
+        load_bytes(0, 1)
         load_x(0)
-        load_bias(0, 2 * HW)
         load_x(1)
-        load_bytes(1)
+        load_bytes(1, 2)
+        load_bias(0, 2 * HW)
         load_bytes(2)
         load_bias(2 * HW, NH * HW)
         for c in range(3, NCH):

@@ -190,8 +190,8 @@ def tile_pgtattention_pa_kernel(tc, hidden_states, W_qkv_bytes, W_qkv_scale, b_q
                                   scales=xs[:, j0:j0 + 2, :].rearrange("p j n -> p (j n)"),
                                   in_=xgrp[b][:, j0:j0 + 2, :].rearrange("p j n -> p (j n)"))
 
-        cosf = const.tile([P, NJ, 2, 16], F32, name="cosf")
-        sinf = const.tile([P, NJ, 2, 16], F32, name="sinf")
+        table = const.tile([P, NJ, 4, 16], F32, name="table")
+        tables = const.tile([P, 4 * NJ, 2, 32], F32, name="tables")
         two_pi = 2.0 * math.pi
 
         def small(name):
@@ -250,10 +250,11 @@ def tile_pgtattention_pa_kernel(tc, hidden_states, W_qkv_bytes, W_qkv_scale, b_q
             scaled(c2[:], s4q[:], -2.0, 1.0, eng)
             s2d = small("s2d")
             scaled(s2d[:], s2[:], 2.0, 0.0, eng)
-            both = [P, NJ, 2, 16]
-            scaled(cosf[:], s2q[:].unsqueeze(2).to_broadcast(both), -2.0, 1.0, eng)
-            eng.tensor_tensor(out=sinf[:], in0=s2d[:].unsqueeze(2).to_broadcast(both), in1=c2[:].unsqueeze(2).to_broadcast(both),
-                              op=ALU.mult)
+            scaled(table[:, :, 0:2, :], s2q[:].unsqueeze(2).to_broadcast([P, NJ, 2, 16]), -2.0, 1.0, eng)
+            eng.tensor_tensor(out=table[:, :, 2, :], in0=s2d[:], in1=c2[:], op=ALU.mult)
+            scaled(table[:, :, 3, :], table[:, :, 2, :], -1.0, 0.0, eng)
+            scaled(tables[:].rearrange("p (k j) a i -> p k (j a i)", k=4),
+                   table[:].rearrange("p j q i -> p (j q i)").unsqueeze(1).to_broadcast([P, 4, NJ * 64]), 1.0, 0.0, eng)
 
         res = {}
         acc = {}
@@ -283,7 +284,7 @@ def tile_pgtattention_pa_kernel(tc, hidden_states, W_qkv_bytes, W_qkv_scale, b_q
             else:
                 head, part = h0 + k, 2
             nc.sync.dma_start(out=outs[part][b, head].rearrange("(p j) d -> p (j d)", j=NJ),
-                              in_=res[i][:, k, b, :, :].rearrange("p j d -> p (j d)"))
+                              in_=res[i][:, b, k, :, :].rearrange("p j d -> p (j d)"))
 
         def evac(i, b):
             c, kind = PIECES[i]
@@ -291,10 +292,10 @@ def tile_pgtattention_pa_kernel(tc, hidden_states, W_qkv_bytes, W_qkv_scale, b_q
             nk = blocks_of(i)
             per = 4 // nk
             if i not in res:
-                res[i] = resp.tile([P, nk, NB, NJ, HD], F32, name="res_%d" % i, tag="res%d" % kind)
+                res[i] = resp.tile([P, NB, nk, NJ, HD], F32, name="res_%d" % i, tag="res%d" % kind)
             if per == 1:
                 for j in range(NJ):
-                    nc.vector.tensor_tensor(out=res[i][:, :, b, j, :].rearrange("p (h q) d -> p h q d", h=2),
+                    nc.vector.tensor_tensor(out=res[i][:, b, :, j, :].rearrange("p (h q) d -> p h q d", h=2),
                                             in0=bias_heads[:, h0:h0 + 2, 0:256].rearrange("p h (q d) -> p h q d", q=2),
                                             in1=acc[(i, b, j)][:].rearrange("p (h q d) -> p h q d", h=2, q=2),
                                             op=ALU.add)
@@ -304,7 +305,7 @@ def tile_pgtattention_pa_kernel(tc, hidden_states, W_qkv_bytes, W_qkv_scale, b_q
                 else:
                     bias = bias_heads[:, h0:h0 + nh, 256:HW]
                 for jj in range(NJ // per):
-                    nc.vector.tensor_tensor(out=res[i][:, :, b, per * jj:per * (jj + 1), :].rearrange("p k j d -> p j k d"),
+                    nc.vector.tensor_tensor(out=res[i][:, b, :, per * jj:per * (jj + 1), :].rearrange("p k j d -> p j k d"),
                                             in0=bias.unsqueeze(1).to_broadcast([P, per, nk, HD]),
                                             in1=acc[(i, b, jj)][:].rearrange("p (j k d) -> p j k d", j=per, k=nk),
                                             op=ALU.add)
@@ -315,22 +316,21 @@ def tile_pgtattention_pa_kernel(tc, hidden_states, W_qkv_bytes, W_qkv_scale, b_q
 
         prod = {}
 
+        def rotated(i, b):
+            return res[i][:, b, :, :, :].rearrange("p k j d -> p (k j) d")[:, :, 0:32]
+
         def rope_products(i, b, eng):
-            n = blocks_of(i)
-            u = scr.tile([P, n, NJ, 32], F32, name="u_%d_%d" % (i, b), tag="u%d" % b)
-            v = scr.tile([P, n, NJ, 32], F32, name="v_%d_%d" % (i, b), tag="v%d" % b)
-            prod[(i, b)] = (u, v)
-            x = res[i][:, :, b, :, 0:32]
-            shape = [P, n, NJ, 32]
-            eng.tensor_tensor(out=u[:], in0=x, in1=cosf[:].rearrange("p j h i -> p j (h i)").unsqueeze(1).to_broadcast(shape),
-                              op=ALU.mult)
-            eng.tensor_tensor(out=v[:], in0=x, in1=sinf[:].rearrange("p j h i -> p j (h i)").unsqueeze(1).to_broadcast(shape),
-                              op=ALU.mult)
+            rows = blocks_of(i) * NJ
+            pr = scr.tile([P, rows, 2, 32], F32, name="pr_%d_%d" % (i, b), tag="pr%d" % b)
+            prod[(i, b)] = pr
+            eng.tensor_tensor(out=pr[:], in0=rotated(i, b).unsqueeze(2).to_broadcast([P, rows, 2, 32]),
+                              in1=tables[:, 0:rows, :, :], op=ALU.mult)
 
         def rope_sums(i, b, eng):
-            u, v = prod[(i, b)]
-            eng.tensor_tensor(out=res[i][:, :, b, :, 0:16], in0=u[:, :, :, 0:16], in1=v[:, :, :, 16:32], op=ALU.subtract)
-            eng.tensor_tensor(out=res[i][:, :, b, :, 16:32], in0=u[:, :, :, 16:32], in1=v[:, :, :, 0:16], op=ALU.add)
+            pr = prod[(i, b)]
+            eng.tensor_tensor(out=rotated(i, b).rearrange("p r (h i) -> p r h i", h=2),
+                              in0=pr[:, :, 0, :].rearrange("p r (h i) -> p r h i", h=2),
+                              in1=pr[:, :, 1, :].rearrange("p r (h i) -> p r h i", h=2)[:, :, ::-1, :], op=ALU.add)
 
         pos_i = const.tile([P, NJ], I32, name="pos_i")
         nc.gpsimd.iota(pos_i[:], pattern=[[1, NJ]], base=0, channel_multiplier=NJ)

@@ -191,7 +191,6 @@ def tile_pgtattention_pa_kernel(tc, hidden_states, W_qkv_bytes, W_qkv_scale, b_q
                                   in_=xgrp[b][:, j0:j0 + 2, :].rearrange("p j n -> p (j n)"))
 
         table = const.tile([P, NJ, 4, 16], F32, name="table")
-        tables = const.tile([P, 4 * NJ, 2, 32], F32, name="tables")
         two_pi = 2.0 * math.pi
 
         def small(name):
@@ -253,8 +252,6 @@ def tile_pgtattention_pa_kernel(tc, hidden_states, W_qkv_bytes, W_qkv_scale, b_q
             scaled(table[:, :, 0:2, :], s2q[:].unsqueeze(2).to_broadcast([P, NJ, 2, 16]), -2.0, 1.0, eng)
             eng.tensor_tensor(out=table[:, :, 2, :], in0=s2d[:], in1=c2[:], op=ALU.mult)
             scaled(table[:, :, 3, :], table[:, :, 2, :], -1.0, 0.0, eng)
-            scaled(tables[:].rearrange("p (k j) a i -> p k (j a i)", k=4),
-                   table[:].rearrange("p j q i -> p (j q i)").unsqueeze(1).to_broadcast([P, 4, NJ * 64]), 1.0, 0.0, eng)
 
         res = {}
         acc = {}
@@ -320,11 +317,13 @@ def tile_pgtattention_pa_kernel(tc, hidden_states, W_qkv_bytes, W_qkv_scale, b_q
             return res[i][:, b, :, :, :].rearrange("p k j d -> p (k j) d")[:, :, 0:32]
 
         def rope_products(i, b, eng):
-            rows = blocks_of(i) * NJ
-            pr = scr.tile([P, rows, 2, 32], F32, name="pr_%d_%d" % (i, b), tag="pr%d" % b)
+            nk = blocks_of(i)
+            pr = scr.tile([P, nk * NJ, 2, 32], F32, name="pr_%d_%d" % (i, b), tag="pr%d" % b)
             prod[(i, b)] = pr
-            eng.tensor_tensor(out=pr[:], in0=rotated(i, b).unsqueeze(2).to_broadcast([P, rows, 2, 32]),
-                              in1=tables[:, 0:rows, :, :], op=ALU.mult)
+            shape = [P, nk, NJ, 2, 32]
+            eng.tensor_tensor(out=pr[:].rearrange("p (k j) a i -> p k j a i", k=nk),
+                              in0=res[i][:, b, :, :, 0:32].unsqueeze(3).to_broadcast(shape),
+                              in1=table[:].rearrange("p j (a h) i -> p j a (h i)", a=2).unsqueeze(1).to_broadcast(shape), op=ALU.mult)
 
         def rope_sums(i, b, eng):
             pr = prod[(i, b)]

@@ -363,7 +363,8 @@ def tile_pgtattention_pa_kernel(tc, hidden_states, W_qkv_bytes, W_qkv_scale, b_q
         quant(1)
         x_quant(1, 0)
         x_quant(1, 2)
-        mm(0, 1)
+        mm(1, 0)
+        mm(1, 1)
         widen(1, 0, False)
         interleave(2, 0, True)
         interleave(3, 0, True)
@@ -387,25 +388,25 @@ def tile_pgtattention_pa_kernel(tc, hidden_states, W_qkv_bytes, W_qkv_scale, b_q
                 rope_sums(qk - 2, 1, nc.gpsimd)
             rope_products(qk, 0, nc.gpsimd)
             rope_sums(qk, 0, nc.gpsimd)
-            mm(vv, 0)
-            mm(vv, 1)
+            mm(qk, 1)
             if not last:
                 keep_warm(4 * CHUNKS[c][1], 1)
-            evac(qk, 1)
             if c > 0:
                 stores(qk - 2, 1)
             evac(vv, 0)
             stores(vv, 0)
             evac(vv, 1)
             stores(vv, 1)
+            evac(qk, 1)
             stores(qk, 0)
             if not last:
                 prepare(qk + 2)
                 quant(qk + 2)
                 mm(qk + 2, 0)
-                mm(qk + 2, 1)
                 prepare(vv + 2)
                 quant(vv + 2)
+                mm(vv + 2, 0)
+                mm(vv + 2, 1)
             rope_products(qk, 1, nc.vector)
             if last:
                 rope_sums(qk, 1, nc.vector)

@@ -240,7 +240,7 @@ def tile_pgtattention_pa_kernel(tc, hidden_states, W_qkv_bytes, W_qkv_scale, b_q
             nc.scalar.activation(out=s4[:], in_=red2[:], func=ACT.Sin, scale=0.25)
 
         def rope_tables():
-            eng = nc.gpsimd
+            eng = nc.vector
             s4q = small("s4q")
             eng.tensor_tensor(out=s4q[:], in0=s4[:], in1=s4[:], op=ALU.mult)
             s2q = small("s2q")
@@ -341,7 +341,6 @@ def tile_pgtattention_pa_kernel(tc, hidden_states, W_qkv_bytes, W_qkv_scale, b_q
             angle_step(8 + t)
         widen(0, 1, False)
         rope_sines()
-        rope_tables()
         keep_warm(1, 16)
         for j in range(NJ):
             x_transpose(0, j)
@@ -349,6 +348,7 @@ def tile_pgtattention_pa_kernel(tc, hidden_states, W_qkv_bytes, W_qkv_scale, b_q
         for j in range(NJ):
             x_evac(0, j)
         interleave(0, 1)
+        rope_tables()
         quant(0)
         x_quant(0, 0)
         x_quant(0, 2)
@@ -360,8 +360,8 @@ def tile_pgtattention_pa_kernel(tc, hidden_states, W_qkv_bytes, W_qkv_scale, b_q
         mm(0, 0)
         interleave(1, 0)
         interleave(1, 1)
-        quant(1)
         x_quant(1, 0)
+        quant(1)
         x_quant(1, 2)
         mm(1, 0)
         mm(1, 1)

@@ -30,7 +30,8 @@ NCH = len(CHUNKS)
 PIECES = tuple((c, kind) for c in range(NCH) for kind in range(2))
 NP = len(PIECES)
 INTER_ON_VECTOR = ((0, 0), (0, 1), (1, 0), (1, 1), (2, 0), (2, 1))
-INTER_ON_GPSIMD = ((2, 0, 0), (3, 0, 0))
+INTER_ON_GPSIMD = ((2, 0, 0), (3, 0, 0), (4, 0, 0), (5, 0, 0), (6, 0, 0))
+INTER_ON_SCALAR = ((2, 1, 1),)
 
 
 def tile_pgtattention_pa_kernel(tc, hidden_states, W_qkv_bytes, W_qkv_scale, b_qkv, out_0, out_1, out_2):
@@ -146,7 +147,7 @@ def tile_pgtattention_pa_kernel(tc, hidden_states, W_qkv_bytes, W_qkv_scale, b_q
                     nc.gpsimd.tensor_scalar(out=dst, in0=src, scalar1=1.0, scalar2=0.0, op0=ALU.mult, op1=ALU.add)
                 elif early:
                     continue
-                elif (i, g) in INTER_ON_VECTOR:
+                elif (i, g) in INTER_ON_VECTOR and (i, g, h) not in INTER_ON_SCALAR:
                     nc.vector.tensor_copy(out=dst, in_=src)
                 else:
                     nc.scalar.copy(out=dst, in_=src)
@@ -374,7 +375,6 @@ def tile_pgtattention_pa_kernel(tc, hidden_states, W_qkv_bytes, W_qkv_scale, b_q
         def prepare(i):
             c = PIECES[i][0]
             if c not in widened:
-                widen(c, 0, False)
                 widen(c, 1, False)
                 widened.append(c)
             interleave(i, 0)
@@ -386,8 +386,13 @@ def tile_pgtattention_pa_kernel(tc, hidden_states, W_qkv_bytes, W_qkv_scale, b_q
             evac(qk, 0)
             if c > 0:
                 rope_sums(qk - 2, 1, nc.gpsimd)
+            if c > 0 and not last:
+                widen(c + 1, 0, False)
+                interleave(qk + 2, 0, True)
             rope_products(qk, 0, nc.gpsimd)
             rope_sums(qk, 0, nc.gpsimd)
+            if c > 0 and not last:
+                interleave(vv + 2, 0, True)
             mm(qk, 1)
             if not last:
                 keep_warm(4 * CHUNKS[c][1], 1)

@@ -52,17 +52,17 @@ def tile_pgtattention_pa_kernel(tc, hidden_states, W_qkv_bytes, W_qkv_scale, b_q
         wview = W_qkv_bytes.rearrange("(g p t) n -> g p t n", g=NG, p=P, t=4)
         wbytes = {}
 
-        def load_bytes(c, by_plane=0):
+        def load_bytes(c, by_plane=0, passes=(0, 1)):
             h0, nh = CHUNKS[c]
             lo, hi = h0 * HW, (h0 + nh) * HW
-            for g in range(NG):
+            for g in passes:
                 wbytes[(c, g)] = const.tile([P, 4, hi - lo], U8, name="wbytes_%d_%d" % (c, g))
             if by_plane == 1:
                 for t in range(4):
                     for g in range(NG):
                         nc.sync.dma_start(out=wbytes[(c, g)][:, t, :], in_=wview[g][:, t, lo:hi])
             elif by_plane == 2:
-                for g in range(NG):
+                for g in passes:
                     for t in range(4):
                         nc.sync.dma_start(out=wbytes[(c, g)][:, t, :], in_=wview[g][:, t, lo:hi])
             else:
@@ -86,8 +86,9 @@ def tile_pgtattention_pa_kernel(tc, hidden_states, W_qkv_bytes, W_qkv_scale, b_q
         load_bytes(0, 1)
         load_x(0)
         load_x(1)
-        load_bytes(1, 2)
+        load_bytes(1, 2, (0,))
         load_bias(0, 2 * HW)
+        load_bytes(1, 2, (1,))
         load_bytes(2)
         load_bias(2 * HW, NH * HW)
         for c in range(3, NCH):

@@ -31,7 +31,7 @@ PIECES = tuple((c, kind) for c in range(NCH) for kind in range(2))
 NP = len(PIECES)
 INTER_ON_VECTOR = ((0, 0), (0, 1), (1, 0), (1, 1), (2, 0), (2, 1))
 INTER_ON_GPSIMD = ((2, 0, 0), (3, 0, 0), (4, 0, 0), (5, 0, 0), (6, 0, 0))
-INTER_ON_SCALAR = ((2, 1, 1),)
+INTER_ON_SCALAR = ((2, 1, 0), (2, 1, 1))
 
 
 def tile_pgtattention_pa_kernel(tc, hidden_states, W_qkv_bytes, W_qkv_scale, b_qkv, out_0, out_1, out_2):
@@ -409,11 +409,12 @@ def tile_pgtattention_pa_kernel(tc, hidden_states, W_qkv_bytes, W_qkv_scale, b_q
                 prepare(qk + 2)
                 quant(qk + 2)
                 mm(qk + 2, 0)
+            rope_products(qk, 1, nc.vector)
+            if not last:
                 prepare(vv + 2)
                 quant(vv + 2)
                 mm(vv + 2, 0)
                 mm(vv + 2, 1)
-            rope_products(qk, 1, nc.vector)
             if last:
                 rope_sums(qk, 1, nc.vector)
                 stores(qk, 1)

@@ -29,7 +29,7 @@ CHUNKS = ((0, 2), (2, 2), (4, 2), (6, 1), (7, 1))
 NCH = len(CHUNKS)
 PIECES = tuple((c, kind) for c in range(NCH) for kind in range(2))
 NP = len(PIECES)
-INTER_ON_VECTOR = ((0, 0), (0, 1), (1, 0), (1, 1), (2, 0), (2, 1))
+INTER_ON_VECTOR = ((0, 0), (0, 1), (1, 1), (2, 0), (2, 1))
 INTER_ON_GPSIMD = ((2, 0, 0), (3, 0, 0), (4, 0, 0), (5, 0, 0), (6, 0, 0))
 INTER_ON_SCALAR = ((2, 1, 0), (2, 1, 1))
 
@@ -357,10 +357,10 @@ def tile_pgtattention_pa_kernel(tc, hidden_states, W_qkv_bytes, W_qkv_scale, b_q
         keep_warm(1, 4)
         for j in range(NJ):
             x_transpose(1, j)
+        interleave(1, 0)
         for j in range(NJ):
             x_evac(1, j)
         mm(0, 0)
-        interleave(1, 0)
         interleave(1, 1)
         x_quant(1, 0)
         quant(1)

from contextlib import ExitStack
import math

import concourse.mybir as mybir
from concourse.masks import make_identity

FLOPS = 2 * 1024 * 1024 * 3072

F32 = mybir.dt.float32
BF16 = mybir.dt.bfloat16
U32 = mybir.dt.uint32
U8 = mybir.dt.uint8
I32 = mybir.dt.int32
FP8 = mybir.dt.float8_e4m3fn
FP8X4 = mybir.dt.float8_e4m3fn_x4
ALU = mybir.AluOpType
ACT = mybir.ActivationFunctionType

P = 128
NB = 2
NJ = 4
NG = 2
HD = 128
HW = 384
NH = 8
BASE = 10000.0

CHUNKS = ((0, 2), (2, 2), (4, 2), (6, 1), (7, 1))
NCH = len(CHUNKS)
PIECES = tuple((c, kind) for c in range(NCH) for kind in range(2))
NP = len(PIECES)
INTER_ON_VECTOR = ((0, 0), (0, 1), (1, 1), (2, 0), (2, 1))
INTER_ON_GPSIMD = ((2, 0, 0), (3, 0, 0), (4, 0, 0), (5, 0, 0), (6, 0, 0))
INTER_ON_SCALAR = ((2, 1, 0), (2, 1, 1))


def tile_pgtattention_pa_kernel(tc, hidden_states, W_qkv_bytes, W_qkv_scale, b_qkv, out_0, out_1, out_2):
    nc = tc.nc
    outs = (out_0, out_1, out_2)

    with ExitStack() as ctx:
        ctx.enter_context(tc.manual_schedule())
        const = ctx.enter_context(tc.tile_pool(name="const", bufs=1))
        stage = ctx.enter_context(tc.tile_pool(name="stage", bufs=2))
        codes = ctx.enter_context(tc.tile_pool(name="codes", bufs=3))
        resp = ctx.enter_context(tc.tile_pool(name="resp", bufs=3))
        scr = ctx.enter_context(tc.tile_pool(name="scr", bufs=1))
        psum = ctx.enter_context(tc.psum_pool(name="psum", bufs=8))

        wsc = const.tile([P, NG, 4], F32, name="wsc")
        nc.sync.dma_start(out=wsc[:], in_=W_qkv_scale.rearrange("(g p t) o -> p g (t o)", g=NG, p=P, t=4))
        wview = W_qkv_bytes.rearrange("(g p t) n -> g p t n", g=NG, p=P, t=4)
        wbytes = {}

        def load_bytes(c, by_plane=0, passes=(0, 1)):
            h0, nh = CHUNKS[c]
            lo, hi = h0 * HW, (h0 + nh) * HW
            for g in passes:
                wbytes[(c, g)] = const.tile([P, 4, hi - lo], U8, name="wbytes_%d_%d" % (c, g))
            if by_plane == 1:
                for t in range(4):
                    for g in range(NG):
                        nc.sync.dma_start(out=wbytes[(c, g)][:, t, :], in_=wview[g][:, t, lo:hi])
            elif by_plane == 2:
                for g in passes:
                    for t in range(4):
                        nc.sync.dma_start(out=wbytes[(c, g)][:, t, :], in_=wview[g][:, t, lo:hi])
            else:
                for g in range(NG):
                    nc.sync.dma_start(out=wbytes[(c, g)][:], in_=wview[g][:, :, lo:hi])

        xsb = {}

        def load_x(b):
            xv = hidden_states[b].rearrange("(p j) k -> p j k", j=NJ)
            for j in range(NJ):
                xt = const.tile([P, 1024], BF16, name="xsb_%d_%d" % (b, j))
                nc.sync.dma_start(out=xt[:], in_=xv[:, j, :])
                xsb[(b, j)] = xt

        bias_bf = const.tile([P, NH * HW], BF16, name="bias_bf")

        def load_bias(lo, hi):
            nc.sync.dma_start(out=bias_bf[:, lo:hi], in_=b_qkv[lo:hi].partition_broadcast(P))

        load_bytes(0, 1)
        load_x(0)
        load_x(1)
        load_bytes(1, 2, (0,))
        load_bias(0, 2 * HW)
        load_bytes(1, 2, (1,))
        load_bytes(2)
        load_bias(2 * HW, NH * HW)
        for c in range(3, NCH):
            load_bytes(c)

        warm = const.tile([P, 1], F32, name="warm")
        nc.vector.memset(warm[:], 0.0)
        warm2 = const.tile([P, 1], F32, name="warm2")
        nc.scalar.activation(out=warm2[:], in_=warm[:], func=ACT.Sin)
        ident = const.tile([P, P], F32, name="ident")
        make_identity(nc, ident[:])

        def keep_warm(banks, each):
            for k in range(banks):
                idle = psum.tile([P, 512], F32, name="idle_%d" % len(idles), tag="bank")
                idles.append(idle)
                for n in range(each):
                    nc.tensor.matmul(out=idle[:, 0:P], lhsT=ident[:], rhs=ident[:], start=True, stop=True)

        idles = []

        wide = {}
        grp = {}
        wcodes = {}

        def widen(c, g, on_vector, planes=(0, 1, 2, 3)):
            if c not in wide:
                wide[c] = stage.tile([P, NG, 4, CHUNKS[c][1] * HW], BF16, name="wide_%d" % c, tag="wide")
            for t in planes:
                src = wbytes[(c, g)][:, t, :].bitcast(FP8)
                if on_vector:
                    nc.vector.tensor_scalar(out=wide[c][:, g, t, :], in0=src, scalar1=wsc[:, g, t:t + 1], scalar2=None,
                                            op0=ALU.mult)
                else:
                    nc.scalar.activation(out=wide[c][:, g, t, :], in_=src, func=ACT.Copy, scale=wsc[:, g, t:t + 1])

        def blocks_of(i):
            c, kind = PIECES[i]
            return CHUNKS[c][1] * (2 - kind)

        def width_of(i):
            return HD * blocks_of(i)

        def interleave(i, g, early=False):
            c, kind = PIECES[i]
            width = width_of(i)
            if i not in grp:
                grp[i] = stage.tile([P, NG, width, 4], BF16, name="grp_%d" % i, tag="grp%d" % kind, align_bytes=64)
            lo, hi = (0, 256) if kind == 0 else (256, HW)
            n = hi - lo
            for h in range(CHUNKS[c][1]):
                src = wide[c][:, g, :, h * HW + lo:h * HW + hi].rearrange("p t (c i) -> p c t i", i=8)
                dst = grp[i][:, g, h * n:(h + 1) * n, :].rearrange("p (c i) t -> p c t i", i=8)
                if (i, g, h) in INTER_ON_GPSIMD:
                    if not early:
                        continue
                    nc.gpsimd.tensor_scalar(out=dst, in0=src, scalar1=1.0, scalar2=0.0, op0=ALU.mult, op1=ALU.add)
                elif early:
                    continue
                elif (i, g) in INTER_ON_VECTOR and (i, g, h) not in INTER_ON_SCALAR:
                    nc.vector.tensor_copy(out=dst, in_=src)
                else:
                    nc.scalar.copy(out=dst, in_=src)

        def quant(i):
            width = width_of(i)
            kind = PIECES[i][1]
            wc = codes.tile([P, NG, width], U32, name="wc_%d" % i, tag="wc%d" % kind, align_bytes=64)
            ws = codes.tile([P, NG, width], U8, name="ws_%d" % i, tag="ws%d" % kind, align_bytes=64)
            wcodes[i] = (wc, ws)
            nc.vector.quantize_mx(out=wc[:].rearrange("p g n -> p (g n)").bitcast(FP8X4),
                                  scales=ws[:].rearrange("p g n -> p (g n)"),
                                  in_=grp[i][:].rearrange("p g n t -> p (g n t)"))

        xbank = {}
        xgrp = {}
        xcodes = {}

        def x_transpose(b, j):
            bank = psum.tile([P, 512], F32, name="xbank_%d_%d" % (b, j), tag="bank")
            xbank[(b, j)] = bank
            words = xsb[(b, j)][:].bitcast(F32)
            for g in range(NG):
                for u in range(2):
                    nc.tensor.transpose(bank[:, (2 * g + u) * P:(2 * g + u + 1) * P],
                                        words[:, 256 * g + u:256 * (g + 1):2], ident[:])

        def x_evac(b, j):
            if b not in xgrp:
                xgrp[b] = const.tile([P, NJ, 1024], BF16, name="xg_%d" % b, align_bytes=64)
            nc.scalar.copy(out=xgrp[b][:, j, :].bitcast(F32).rearrange("p (g r u) -> p g r u", g=NG, u=2),
                           in_=xbank[(b, j)][:].rearrange("p (g u r) -> p g r u", g=NG, u=2))

        def x_quant(b, j0):
            if b not in xcodes:
                xc = const.tile([P, NJ, 256], U32, name="xc_%d" % b, align_bytes=64)
                xs = const.tile([P, NJ, 256], U8, name="xs_%d" % b, align_bytes=64)
                xcodes[b] = (xc, xs)
            xc, xs = xcodes[b]
            nc.vector.quantize_mx(out=xc[:, j0:j0 + 2, :].rearrange("p j n -> p (j n)").bitcast(FP8X4),
                                  scales=xs[:, j0:j0 + 2, :].rearrange("p j n -> p (j n)"),
                                  in_=xgrp[b][:, j0:j0 + 2, :].rearrange("p j n -> p (j n)"))

        table = const.tile([P, NJ, 4, 16], F32, name="table")
        two_pi = 2.0 * math.pi

        def small(name):
            return const.tile([P, NJ, 16], F32, name=name)

        def scaled(dst, src, mul, add, eng=None):
            (eng or nc.vector).tensor_scalar(out=dst, in0=src, scalar1=mul, scalar2=add, op0=ALU.mult, op1=ALU.add)

        red2 = small("red2")
        ang = small("ang")
        turn = small("turn")

        pos_f = const.tile([P, NJ], F32, name="pos_f")
        turn_i = const.tile([P, NJ, 16], I32, name="turn_i")
        turn_f = small("turn_f")
        back = small("back")
        red = small("red")
        over = small("over")

        def angle_step(n):
            if n == 0:
                scaled(ang[:, :, 0], pos_f[:], 1.0, 0.0)
            elif n <= 4:
                w = 2 ** (n - 1)
                scaled(ang[:, :, w:2 * w], ang[:, :, 0:w], BASE ** (-w / 16.0), 0.0)
            elif n == 5:
                scaled(turn[:], ang[:], 1.0 / two_pi, 0.0)
            elif n == 6:
                nc.vector.tensor_copy(out=turn_i[:], in_=turn[:])
            elif n == 7:
                nc.vector.tensor_copy(out=turn_f[:], in_=turn_i[:])
            elif n == 8:
                scaled(back[:], turn_f[:], -two_pi, 0.0)
            elif n == 9:
                nc.vector.tensor_tensor(out=red[:], in0=back[:], in1=ang[:], op=ALU.add)
            elif n == 10:
                nc.vector.tensor_scalar(out=over[:], in0=red[:], scalar1=math.pi, scalar2=-two_pi, op0=ALU.is_gt,
                                        op1=ALU.mult)
            else:
                nc.vector.tensor_tensor(out=red2[:], in0=red[:], in1=over[:], op=ALU.add)

        s2 = small("s2")
        s4 = small("s4")

        def rope_sines():
            nc.scalar.activation(out=s2[:], in_=red2[:], func=ACT.Sin, scale=0.5)
            nc.scalar.activation(out=s4[:], in_=red2[:], func=ACT.Sin, scale=0.25)

        def rope_tables():
            eng = nc.vector
            s4q = small("s4q")
            eng.tensor_tensor(out=s4q[:], in0=s4[:], in1=s4[:], op=ALU.mult)
            s2q = small("s2q")
            eng.tensor_tensor(out=s2q[:], in0=s2[:], in1=s2[:], op=ALU.mult)
            c2 = small("c2")
            scaled(c2[:], s4q[:], -2.0, 1.0, eng)
            s2d = small("s2d")
            scaled(s2d[:], s2[:], 2.0, 0.0, eng)
            scaled(table[:, :, 0:2, :], s2q[:].unsqueeze(2).to_broadcast([P, NJ, 2, 16]), -2.0, 1.0, eng)
            eng.tensor_tensor(out=table[:, :, 2, :], in0=s2d[:], in1=c2[:], op=ALU.mult)
            scaled(table[:, :, 3, :], table[:, :, 2, :], -1.0, 0.0, eng)

        res = {}
        acc = {}

        def mm(i, b):
            width = width_of(i)
            per = 512 // width
            xc, xs = xcodes[b]
            wc, ws = wcodes[i]
            for j in range(NJ):
                if j % per == 0:
                    acc[(i, b, j // per)] = psum.tile([P, 512], F32, name="acc_%d_%d_%d" % (i, b, j), tag="bank")
                bank = acc[(i, b, j // per)]
                lo = (j % per) * width
                for g in range(NG):
                    nc.tensor.matmul_mx(out=bank[:, lo:lo + width], lhsT=xc[:, j, g * P:(g + 1) * P].bitcast(FP8X4),
                                        lhsT_scale=xs[:, j, g * P:(g + 1) * P], rhs=wc[:, g, :].bitcast(FP8X4),
                                        rhs_scale=ws[:, g, :], start=(g == 0), stop=(g == NG - 1))

        bias_heads = bias_bf[:].rearrange("p (h x) -> p h x", x=HW)

        def store(i, b, k):
            c, kind = PIECES[i]
            h0 = CHUNKS[c][0]
            if kind == 0:
                head, part = h0 + k // 2, k % 2
            else:
                head, part = h0 + k, 2
            nc.sync.dma_start(out=outs[part][b, head].rearrange("(p j) d -> p (j d)", j=NJ),
                              in_=res[i][:, b, k, :, :].rearrange("p j d -> p (j d)"))

        def evac(i, b):
            c, kind = PIECES[i]
            h0, nh = CHUNKS[c]
            nk = blocks_of(i)
            per = 4 // nk
            if i not in res:
                res[i] = resp.tile([P, NB, nk, NJ, HD], F32, name="res_%d" % i, tag="res%d" % kind)
            if per == 1:
                for j in range(NJ):
                    nc.vector.tensor_tensor(out=res[i][:, b, :, j, :].rearrange("p (h q) d -> p h q d", h=2),
                                            in0=bias_heads[:, h0:h0 + 2, 0:256].rearrange("p h (q d) -> p h q d", q=2),
                                            in1=acc[(i, b, j)][:].rearrange("p (h q d) -> p h q d", h=2, q=2),
                                            op=ALU.add)
            else:
                if kind == 0:
                    bias = bias_heads[:, h0, 0:256].rearrange("p (k d) -> p k d", k=nk)
                else:
                    bias = bias_heads[:, h0:h0 + nh, 256:HW]
                for jj in range(NJ // per):
                    nc.vector.tensor_tensor(out=res[i][:, b, :, per * jj:per * (jj + 1), :].rearrange("p k j d -> p j k d"),
                                            in0=bias.unsqueeze(1).to_broadcast([P, per, nk, HD]),
                                            in1=acc[(i, b, jj)][:].rearrange("p (j k d) -> p j k d", j=per, k=nk),
                                            op=ALU.add)

        def stores(i, b):
            for k in range(blocks_of(i)):
                store(i, b, k)

        prod = {}

        def rotated(i, b):
            return res[i][:, b, :, :, :].rearrange("p k j d -> p (k j) d")[:, :, 0:32]

        def rope_products(i, b, eng):
            nk = blocks_of(i)
            pr = scr.tile([P, nk * NJ, 2, 32], F32, name="pr_%d_%d" % (i, b), tag="pr%d" % b)
            prod[(i, b)] = pr
            shape = [P, nk, NJ, 2, 32]
            eng.tensor_tensor(out=pr[:].rearrange("p (k j) a i -> p k j a i", k=nk),
                              in0=res[i][:, b, :, :, 0:32].unsqueeze(3).to_broadcast(shape),
                              in1=table[:].rearrange("p j (a h) i -> p j a (h i)", a=2).unsqueeze(1).to_broadcast(shape), op=ALU.mult)

        def rope_sums(i, b, eng):
            pr = prod[(i, b)]
            eng.tensor_tensor(out=rotated(i, b).rearrange("p r (h i) -> p r h i", h=2),
                              in0=pr[:, :, 0, :].rearrange("p r (h i) -> p r h i", h=2),
                              in1=pr[:, :, 1, :].rearrange("p r (h i) -> p r h i", h=2)[:, :, ::-1, :], op=ALU.add)

        pos_i = const.tile([P, NJ], I32, name="pos_i")
        nc.gpsimd.iota(pos_i[:], pattern=[[1, NJ]], base=0, channel_multiplier=NJ)
        nc.vector.tensor_copy(out=pos_f[:], in_=pos_i[:])
        for n in range(8):
            angle_step(n)
        for t in range(4):
            widen(0, 0, True, (t,))
            angle_step(8 + t)
        widen(0, 1, False)
        rope_sines()
        keep_warm(1, 16)
        for j in range(NJ):
            x_transpose(0, j)
        interleave(0, 0)
        for j in range(NJ):
            x_evac(0, j)
        interleave(0, 1)
        rope_tables()
        quant(0)
        x_quant(0, 0)
        x_quant(0, 2)
        keep_warm(1, 4)
        for j in range(NJ):
            x_transpose(1, j)
        interleave(1, 0)
        for j in range(NJ):
            x_evac(1, j)
        mm(0, 0)
        interleave(1, 1)
        x_quant(1, 0)
        quant(1)
        x_quant(1, 2)
        mm(1, 0)
        mm(1, 1)
        widen(1, 0, False)
        interleave(2, 0, True)
        interleave(3, 0, True)
        widen(1, 1, False)
        widened = [0, 1]

        def prepare(i):
            c = PIECES[i][0]
            if c not in widened:
                widen(c, 1, False)
                widened.append(c)
            interleave(i, 0)
            interleave(i, 1)

        for c in range(NCH):
            qk, vv = 2 * c, 2 * c + 1
            last = c == NCH - 1
            evac(qk, 0)
            if c > 0:
                rope_sums(qk - 2, 1, nc.gpsimd)
            if c > 0 and not last:
                widen(c + 1, 0, False)
                interleave(qk + 2, 0, True)
            rope_products(qk, 0, nc.gpsimd)
            rope_sums(qk, 0, nc.gpsimd)
            if c > 0 and not last:
                interleave(vv + 2, 0, True)
            mm(qk, 1)
            if not last:
                keep_warm(4 * CHUNKS[c][1], 1)
            if c > 0:
                stores(qk - 2, 1)
            evac(vv, 0)
            stores(vv, 0)
            evac(vv, 1)
            stores(vv, 1)
            evac(qk, 1)
            stores(qk, 0)
            if not last:
                prepare(qk + 2)
                quant(qk + 2)
                mm(qk + 2, 0)
            rope_products(qk, 1, nc.vector)
            if not last:
                prepare(vv + 2)
                quant(vv + 2)
                mm(vv + 2, 0)
                mm(vv + 2, 1)
            if last:
                rope_sums(qk, 1, nc.vector)
                stores(qk, 1)
